import numpy as np
import ml_dtypes


def mxq(x, axis, fmt="e4m3"):
    dtype, down = {"e4m3": (ml_dtypes.float8_e4m3fn, 7), "e5m2": (ml_dtypes.float8_e5m2, 14)}[fmt]
    v = np.moveaxis(np.asarray(x, np.float32).astype(ml_dtypes.bfloat16).astype(np.float64), axis, -1)
    blocks = v.reshape(v.shape[:-1] + (-1, 32))
    amax = np.abs(blocks).max(-1, keepdims=True)
    byte = np.maximum(np.where(amax > 0, np.frexp(amax)[1] - 1 + 127, 0) - down, 1)
    scale = np.exp2(byte - 127.0)
    codes = (blocks / scale).astype(np.float32).astype(dtype).astype(np.float64)
    return np.moveaxis((codes * scale).reshape(v.shape), -1, axis)


WIDE = False


def mx_kscale(k):
    if not WIDE:
        return np.ones(k)
    levels = np.array([20, -20, 10, -10, 0])
    a = np.random.permutation(np.resize(levels, k // 512 * 4)).reshape(k // 512, 4)
    idx = np.arange(k)
    return np.exp2(a[idx // 512, idx % 128 // 32])


BF16 = ml_dtypes.bfloat16


def bf(x):
    return np.asarray(x, np.float32).astype(BF16)


def f64(x):
    return np.asarray(x).astype(np.float64)


B, C, H, W, O, HS, WS, K = 2, 128, 64, 64, 512, 4, 4, 3
PAD = 0
NI, NJ = H // HS, W // WS


def setup_inputs():
    s = mx_kscale(O)
    fan_in = C * K * K
    x = np.random.standard_normal((B, C, H, W))
    weight = np.random.standard_normal((HS, WS, O, C, K, K)) / np.sqrt(fan_in) / s[None, None, :, None, None, None]
    bias = np.random.standard_normal((HS, WS, O)) * 0.5
    g = np.random.standard_normal((B, O, H, W)) * np.exp2(np.random.randint(-12, 1, (B, 1, H, W))) * 4.0 * s[None, :, None, None]
    return {"x": bf(x), "weight": bf(weight), "bias": bf(bias), "grad_out": bf(g)}


def reference(x, weight, bias, grad_out):
    g, weight = f64(grad_out), f64(weight)
    gs = g.reshape(B, O, NI, HS, NJ, WS).transpose(3, 5, 0, 2, 4, 1).reshape(HS, WS, B * NI * NJ, O)
    ws = weight.transpose(0, 1, 2, 4, 5, 3).reshape(HS, WS, O, K * K * C)
    t = mxq(gs, 3, "e5m2") @ mxq(ws, 2, "e4m3")
    ti = t.reshape(HS, WS, B, NI, NJ, K, K, C).transpose(2, 3, 0, 4, 1, 5, 6, 7).reshape(B, H, W, K, K, C)
    gx = np.zeros((B, H, W, C))
    for u in range(K):
        for v in range(K):
            gx[:, u:, v:, :] += ti[:, :H - u, :W - v, u, v, :]
    return gx.transpose(0, 3, 1, 2)

@@ -1,0 +1,168 @@
+import concourse.mybir as mybir
+
+F32 = mybir.dt.float32
+BF16 = mybir.dt.bfloat16
+U32 = mybir.dt.uint32
+U8 = mybir.dt.uint8
+I32 = mybir.dt.int32
+E4M3X4 = mybir.dt.float8_e4m3fn_x4
+E5M2X4 = mybir.dt.float8_e5m2_x4
+
+B, C, H, W, O, HS, WS, K = 2, 128, 64, 64, 512, 4, 4, 3
+NI, NJ = H // HS, W // WS
+P = 128
+PACK = 4
+N_PIX = B * NI * NJ
+I_STEP = B * NJ
+I_CHUNK = 4
+N_CHUNKS = NI // I_CHUNK
+CHUNK_COLS = I_CHUNK * I_STEP
+TAPS = K * K
+W_COLS = TAPS * C
+QUANT_MAX = 4096
+C_VECTOR = 72
+
+FLOPS = 2 * HS * WS * N_PIX * O * W_COLS
+BYTES = 2 * HS * WS * O * W_COLS + 2 * B * O * H * W + 4 * B * C * H * W
+
+
+def tile_patternconv_t_kernel(tc, x, weight, bias, grad_out, out):
+    nc = tc.nc
+    with tc.tile_pool(name="grad_mx", bufs=1) as grad_mx, tc.tile_pool(name="w_raw", bufs=3) as w_raw_pool, tc.tile_pool(
+        name="w_grouped", bufs=2
+    ) as w_grouped_pool, tc.tile_pool(name="w_mx", bufs=8) as w_mx, tc.psum_pool(name="psum", bufs=8) as psum:
+        g_codes = grad_mx.tile([P, HS * WS, I_STEP + N_PIX], U32, align_bytes=64)
+        g_scales = grad_mx.tile([P, HS * WS, N_PIX], U8, align_bytes=64)
+        g_scales_down = grad_mx.tile([P, 2 * WS, N_PIX], U8, align_bytes=64)
+        nc.vector.memset(g_codes[:, :, 0:I_STEP].bitcast(I32), 0)
+        nc.vector.memset(g_scales[:].bitcast(I32), 0)
+        nc.vector.memset(g_scales_down[:].bitcast(I32), 0)
+
+        with tc.tile_pool(name="g_raw", bufs=2) as g_raw_pool, tc.tile_pool(name="g_grouped", bufs=2) as g_grouped_pool:
+            for m in range(N_CHUNKS):
+                rows = slice(m * I_CHUNK * HS, (m + 1) * I_CHUNK * HS)
+                g_raw = g_raw_pool.tile([P, B, PACK, I_CHUNK * HS * W], BF16)
+                for b in range(B):
+                    nc.sync.dma_start(
+                        out=g_raw[:, b], in_=grad_out[b, :, rows, :].rearrange("(p t) y z -> p t (y z)", t=PACK)
+                    )
+                g_grouped = g_grouped_pool.tile([P, HS, WS, I_CHUNK, B, NJ, PACK], BF16, align_bytes=64)
+                for b in range(B):
+                    by_place = g_raw[:, b].rearrange("p t (i h j w) -> p h i j t w", i=I_CHUNK, h=HS, j=NJ, w=WS)
+                    for h in range(HS):
+                        dst = g_grouped[:, h, :, :, b, :, :].rearrange("p w i j t -> p i j t w")
+                        if h < HS // 2:
+                            nc.vector.tensor_copy(out=dst, in_=by_place[:, h])
+                        else:
+                            for i in range(I_CHUNK):
+                                nc.scalar.copy(out=dst[:, i], in_=by_place[:, h, i])
+                for place in range(HS * WS):
+                    cols = slice(m * CHUNK_COLS, (m + 1) * CHUNK_COLS)
+                    padded_cols = slice(I_STEP + m * CHUNK_COLS, I_STEP + (m + 1) * CHUNK_COLS)
+                    nc.vector.quantize_mx(
+                        out=g_codes[:, place, padded_cols].bitcast(E5M2X4),
+                        scales=g_scales[:, place, cols],
+                        in_=g_grouped[:, place // WS, place % WS].rearrange("p i b j t -> p (i b j t)"),
+                    )
+            for low_place in range(2 * WS):
+                nc.vector.tensor_copy(
+                    out=g_scales_down[:, low_place, I_STEP:N_PIX].bitcast(I32),
+                    in_=g_scales[:, 2 * WS + low_place, 0 : N_PIX - I_STEP].bitcast(I32),
+                )
+
+        with tc.tile_pool(name="planes", bufs=1) as planes_pool, tc.tile_pool(name="out_sb", bufs=2) as out_pool:
+            planes = planes_pool.tile([P, HS, WS, NI, B, NJ], F32)
+            open_groups = {}
+            passes_done = {}
+
+            def prepare_weights(h_src, w_src):
+                w_raw = w_raw_pool.tile([P, PACK, C, K, K], BF16)
+                nc.sync.dma_start(
+                    out=w_raw[:].rearrange("p t c u v -> p (t c u v)"),
+                    in_=weight[h_src, w_src].rearrange("(p t) c u v -> p (t c u v)", t=PACK),
+                )
+                w_grouped = w_grouped_pool.tile([P, K, K, C, PACK], BF16, align_bytes=64)
+                for u in range(K):
+                    nc.vector.tensor_copy(
+                        out=w_grouped[:, u, :, 0:C_VECTOR, :].rearrange("p v c t -> p c t v"),
+                        in_=w_raw[:, :, 0:C_VECTOR, u, :].rearrange("p t c v -> p c t v"),
+                    )
+                    nc.scalar.copy(
+                        out=w_grouped[:, u, :, C_VECTOR:C, :].rearrange("p v c t -> p c t v"),
+                        in_=w_raw[:, :, C_VECTOR:C, u, :].rearrange("p t c v -> p c t v"),
+                    )
+                w_codes = w_mx.tile([P, W_COLS], U32, align_bytes=64)
+                w_scales = w_mx.tile([P, W_COLS], U8, align_bytes=64)
+                flat = w_grouped[:].rearrange("p u v c t -> p (u v c t)")
+                for first in (0, QUANT_MAX // PACK):
+                    last = min(first + QUANT_MAX // PACK, W_COLS)
+                    nc.vector.quantize_mx(
+                        out=w_codes[:, first:last].bitcast(E4M3X4),
+                        scales=w_scales[:, first:last],
+                        in_=flat[:, first * PACK : last * PACK],
+                    )
+                return w_codes, w_scales
+
+            def close_group(hy, wz, dj, acc):
+                plane = planes[:, hy, wz]
+                if dj == 0:
+                    nc.scalar.copy(out=plane.rearrange("p i b j -> p (i b j)"), in_=acc[:])
+                else:
+                    shifted = acc[:].rearrange("p (i b j) -> p i b j", i=NI, b=B)
+                    nc.vector.tensor_add(
+                        out=plane[:, :, :, 1:NJ], in0=shifted[:, :, :, 0 : NJ - 1], in1=plane[:, :, :, 1:NJ]
+                    )
+
+            def add_passes(h_src, w_src, v, w_codes, w_scales):
+                wz, dj = (w_src + v) % WS, (w_src + v) // WS
+                source_columns = min(wz + 1, K) if dj == 0 else K - 1 - wz
+                for u in range(K):
+                    hy, di = (h_src + u) % HS, (h_src + u) // HS
+                    key = (hy, wz, dj)
+                    if key not in open_groups:
+                        acc = psum.tile([P, N_PIX], F32)
+                        open_groups[key] = acc
+                        passes_done[key] = 0
+                    acc = open_groups[key]
+                    place = h_src * WS + w_src
+                    if di == 0:
+                        rhs = g_codes[:, place, I_STEP : I_STEP + N_PIX]
+                        rhs_scale = g_scales[:, place, :]
+                    else:
+                        rhs = g_codes[:, place, 0:N_PIX]
+                        rhs_scale = g_scales_down[:, place - 2 * WS, :]
+                    tap = slice((u * K + v) * C, (u * K + v + 1) * C)
+                    passes_done[key] += 1
+                    nc.tensor.matmul_mx(
+                        out=acc[:],
+                        lhsT=w_codes[:, tap].bitcast(E4M3X4),
+                        lhsT_scale=w_scales[:, tap],
+                        rhs=rhs.bitcast(E5M2X4),
+                        rhs_scale=rhs_scale,
+                        start=(passes_done[key] == 1),
+                        stop=(passes_done[key] == K * source_columns),
+                    )
+                    if passes_done[key] == K * source_columns:
+                        close_group(hy, wz, dj, acc)
+
+            for w_src in range(WS):
+                column = []
+                for h_src in range(HS):
+                    w_codes, w_scales = prepare_weights(h_src, w_src)
+                    column.append((w_codes, w_scales))
+                    for v in range(K - 1):
+                        add_passes(h_src, w_src, v, w_codes, w_scales)
+                for h_src in range(HS):
+                    add_passes(h_src, w_src, K - 1, column[h_src][0], column[h_src][1])
+
+            for b in range(B):
+                out_sb = out_pool.tile([P, NI, HS, NJ, WS], F32)
+                for hy in range(HS):
+                    src = planes[:, hy, :, :, b, :].rearrange("p w i j -> p i j w")
+                    if hy < HS - 1:
+                        nc.vector.tensor_copy(out=out_sb[:, :, hy, :, :], in_=src)
+                    else:
+                        nc.scalar.copy(out=out_sb[:, :, hy, :, :], in_=src)
+                nc.sync.dma_start(
+                    out=out[b].rearrange("c y z -> c (y z)"), in_=out_sb[:].rearrange("p i h j w -> p (i h j w)")
+                )

@@ -20,7 +20,10 @@ CHUNK_COLS = I_CHUNK * I_STEP
 TAPS = K * K
 W_COLS = TAPS * C
 QUANT_MAX = 4096
-C_VECTOR = 72
+H_VECTOR = 3
+C_VECTOR_FIRST = 8
+C_VECTOR = 60
+I_STORE = 8
 
 FLOPS = 2 * HS * WS * N_PIX * O * W_COLS
 BYTES = 2 * HS * WS * O * W_COLS + 2 * B * O * H * W + 4 * B * C * H * W
@@ -28,18 +31,51 @@ BYTES = 2 * HS * WS * O * W_COLS + 2 * B * O * H * W + 4 * B * C * H * W
 
 def tile_patternconv_t_kernel(tc, x, weight, bias, grad_out, out):
     nc = tc.nc
-    with tc.tile_pool(name="grad_mx", bufs=1) as grad_mx, tc.tile_pool(name="w_raw", bufs=3) as w_raw_pool, tc.tile_pool(
+    with tc.tile_pool(name="keep", bufs=1) as keep, tc.tile_pool(name="w_raw", bufs=3) as w_raw_pool, tc.tile_pool(
         name="w_grouped", bufs=2
     ) as w_grouped_pool, tc.tile_pool(name="w_mx", bufs=8) as w_mx, tc.psum_pool(name="psum", bufs=8) as psum:
-        g_codes = grad_mx.tile([P, HS * WS, I_STEP + N_PIX], U32, align_bytes=64)
-        g_scales = grad_mx.tile([P, HS * WS, N_PIX], U8, align_bytes=64)
-        g_scales_down = grad_mx.tile([P, 2 * WS, N_PIX], U8, align_bytes=64)
+        g_codes = keep.tile([P, HS * WS, I_STEP + N_PIX], U32, align_bytes=64)
+        g_scales = keep.tile([P, HS * WS, N_PIX], U8, align_bytes=64)
+        g_scales_down = keep.tile([P, 2 * WS, N_PIX], U8, align_bytes=64)
         nc.vector.memset(g_codes[:, :, 0:I_STEP].bitcast(I32), 0)
         nc.vector.memset(g_scales[:].bitcast(I32), 0)
         nc.vector.memset(g_scales_down[:].bitcast(I32), 0)
+        quantised = {}
+
+        def regroup_weights(h_src, w_src, c_vector):
+            w_raw = w_raw_pool.tile([P, PACK, C, K, K], BF16)
+            nc.sync.dma_start(
+                out=w_raw[:].rearrange("p t c u v -> p (t c u v)"),
+                in_=weight[h_src, w_src].rearrange("(p t) c u v -> p (t c u v)", t=PACK),
+            )
+            w_grouped = w_grouped_pool.tile([P, K, K, C, PACK], BF16, align_bytes=64)
+            for u in range(K):
+                nc.vector.tensor_copy(
+                    out=w_grouped[:, u, :, 0:c_vector, :].rearrange("p v c t -> p c t v"),
+                    in_=w_raw[:, :, 0:c_vector, u, :].rearrange("p t c v -> p c t v"),
+                )
+                nc.scalar.copy(
+                    out=w_grouped[:, u, :, c_vector:C, :].rearrange("p v c t -> p c t v"),
+                    in_=w_raw[:, :, c_vector:C, u, :].rearrange("p t c v -> p c t v"),
+                )
+            return w_grouped
+
+        def quantise_weights(h_src, w_src, w_grouped):
+            w_codes = w_mx.tile([P, W_COLS], U32, align_bytes=64)
+            w_scales = w_mx.tile([P, W_COLS], U8, align_bytes=64)
+            flat = w_grouped[:].rearrange("p u v c t -> p (u v c t)")
+            for first in (0, QUANT_MAX // PACK):
+                last = min(first + QUANT_MAX // PACK, W_COLS)
+                nc.vector.quantize_mx(
+                    out=w_codes[:, first:last].bitcast(E4M3X4),
+                    scales=w_scales[:, first:last],
+                    in_=flat[:, first * PACK : last * PACK],
+                )
+            quantised[(h_src, w_src)] = (w_codes, w_scales)
 
         with tc.tile_pool(name="g_raw", bufs=2) as g_raw_pool, tc.tile_pool(name="g_grouped", bufs=2) as g_grouped_pool:
-            for m in range(N_CHUNKS):
+
+            def regroup_grad(m):
                 rows = slice(m * I_CHUNK * HS, (m + 1) * I_CHUNK * HS)
                 g_raw = g_raw_pool.tile([P, B, PACK, I_CHUNK * HS * W], BF16)
                 for b in range(B):
@@ -51,11 +87,14 @@ def tile_patternconv_t_kernel(tc, x, weight, bias, grad_out, out):
                     by_place = g_raw[:, b].rearrange("p t (i h j w) -> p h i j t w", i=I_CHUNK, h=HS, j=NJ, w=WS)
                     for h in range(HS):
                         dst = g_grouped[:, h, :, :, b, :, :].rearrange("p w i j t -> p i j t w")
-                        if h < HS // 2:
+                        if h < H_VECTOR:
                             nc.vector.tensor_copy(out=dst, in_=by_place[:, h])
                         else:
                             for i in range(I_CHUNK):
                                 nc.scalar.copy(out=dst[:, i], in_=by_place[:, h, i])
+                return g_grouped
+
+            def quantise_grad(m, g_grouped):
                 for place in range(HS * WS):
                     cols = slice(m * CHUNK_COLS, (m + 1) * CHUNK_COLS)
                     padded_cols = slice(I_STEP + m * CHUNK_COLS, I_STEP + (m + 1) * CHUNK_COLS)
@@ -64,44 +103,25 @@ def tile_patternconv_t_kernel(tc, x, weight, bias, grad_out, out):
                         scales=g_scales[:, place, cols],
                         in_=g_grouped[:, place // WS, place % WS].rearrange("p i b j t -> p (i b j t)"),
                     )
+
+            assert N_CHUNKS == HS
+            grouped = {}
+            for m in range(N_CHUNKS + 1):
+                if m < N_CHUNKS:
+                    grouped[m] = (regroup_grad(m), regroup_weights(m, 0, C_VECTOR_FIRST))
+                if m > 0:
+                    quantise_grad(m - 1, grouped[m - 1][0])
+                    quantise_weights(m - 1, 0, grouped[m - 1][1])
             for low_place in range(2 * WS):
                 nc.vector.tensor_copy(
                     out=g_scales_down[:, low_place, I_STEP:N_PIX].bitcast(I32),
                     in_=g_scales[:, 2 * WS + low_place, 0 : N_PIX - I_STEP].bitcast(I32),
                 )
 
-        with tc.tile_pool(name="planes", bufs=1) as planes_pool, tc.tile_pool(name="out_sb", bufs=2) as out_pool:
+        with tc.tile_pool(name="planes", bufs=1) as planes_pool, tc.tile_pool(name="out_sb", bufs=4) as out_pool:
             planes = planes_pool.tile([P, HS, WS, NI, B, NJ], F32)
             open_groups = {}
             passes_done = {}
-
-            def prepare_weights(h_src, w_src):
-                w_raw = w_raw_pool.tile([P, PACK, C, K, K], BF16)
-                nc.sync.dma_start(
-                    out=w_raw[:].rearrange("p t c u v -> p (t c u v)"),
-                    in_=weight[h_src, w_src].rearrange("(p t) c u v -> p (t c u v)", t=PACK),
-                )
-                w_grouped = w_grouped_pool.tile([P, K, K, C, PACK], BF16, align_bytes=64)
-                for u in range(K):
-                    nc.vector.tensor_copy(
-                        out=w_grouped[:, u, :, 0:C_VECTOR, :].rearrange("p v c t -> p c t v"),
-                        in_=w_raw[:, :, 0:C_VECTOR, u, :].rearrange("p t c v -> p c t v"),
-                    )
-                    nc.scalar.copy(
-                        out=w_grouped[:, u, :, C_VECTOR:C, :].rearrange("p v c t -> p c t v"),
-                        in_=w_raw[:, :, C_VECTOR:C, u, :].rearrange("p t c v -> p c t v"),
-                    )
-                w_codes = w_mx.tile([P, W_COLS], U32, align_bytes=64)
-                w_scales = w_mx.tile([P, W_COLS], U8, align_bytes=64)
-                flat = w_grouped[:].rearrange("p u v c t -> p (u v c t)")
-                for first in (0, QUANT_MAX // PACK):
-                    last = min(first + QUANT_MAX // PACK, W_COLS)
-                    nc.vector.quantize_mx(
-                        out=w_codes[:, first:last].bitcast(E4M3X4),
-                        scales=w_scales[:, first:last],
-                        in_=flat[:, first * PACK : last * PACK],
-                    )
-                return w_codes, w_scales
 
             def close_group(hy, wz, dj, acc):
                 plane = planes[:, hy, wz]
@@ -113,7 +133,8 @@ def tile_patternconv_t_kernel(tc, x, weight, bias, grad_out, out):
                         out=plane[:, :, :, 1:NJ], in0=shifted[:, :, :, 0 : NJ - 1], in1=plane[:, :, :, 1:NJ]
                     )
 
-            def add_passes(h_src, w_src, v, w_codes, w_scales):
+            def add_passes(h_src, w_src, v):
+                w_codes, w_scales = quantised[(h_src, w_src)]
                 wz, dj = (w_src + v) % WS, (w_src + v) // WS
                 source_columns = min(wz + 1, K) if dj == 0 else K - 1 - wz
                 for u in range(K):
@@ -145,24 +166,34 @@ def tile_patternconv_t_kernel(tc, x, weight, bias, grad_out, out):
                     if passes_done[key] == K * source_columns:
                         close_group(hy, wz, dj, acc)
 
-            for w_src in range(WS):
-                column = []
-                for h_src in range(HS):
-                    w_codes, w_scales = prepare_weights(h_src, w_src)
-                    column.append((w_codes, w_scales))
-                    for v in range(K - 1):
-                        add_passes(h_src, w_src, v, w_codes, w_scales)
-                for h_src in range(HS):
-                    add_passes(h_src, w_src, K - 1, column[h_src][0], column[h_src][1])
+            def multiply(h_src, w_src):
+                for v in range(K - 1):
+                    add_passes(h_src, w_src, v)
+                if h_src == HS - 1:
+                    for h_again in range(HS):
+                        add_passes(h_again, w_src, K - 1)
+
+            for h_src in range(HS):
+                multiply(h_src, 0)
+            places = [(h_src, w_src) for w_src in range(1, WS) for h_src in range(HS)]
+            w_grouped_of = {}
+            for n in range(len(places) + 1):
+                if n < len(places):
+                    w_grouped_of[n] = regroup_weights(places[n][0], places[n][1], C_VECTOR)
+                if n > 0:
+                    quantise_weights(places[n - 1][0], places[n - 1][1], w_grouped_of[n - 1])
+                    multiply(places[n - 1][0], places[n - 1][1])
 
             for b in range(B):
-                out_sb = out_pool.tile([P, NI, HS, NJ, WS], F32)
-                for hy in range(HS):
-                    src = planes[:, hy, :, :, b, :].rearrange("p w i j -> p i j w")
-                    if hy < HS - 1:
-                        nc.vector.tensor_copy(out=out_sb[:, :, hy, :, :], in_=src)
-                    else:
-                        nc.scalar.copy(out=out_sb[:, :, hy, :, :], in_=src)
-                nc.sync.dma_start(
-                    out=out[b].rearrange("c y z -> c (y z)"), in_=out_sb[:].rearrange("p i h j w -> p (i h j w)")
-                )
+                for i_first in range(0, NI, I_STORE):
+                    out_sb = out_pool.tile([P, I_STORE, HS, NJ, WS], F32)
+                    for hy in range(HS):
+                        src = planes[:, hy, :, i_first : i_first + I_STORE, b, :].rearrange("p w i j -> p i j w")
+                        if hy < HS - 1:
+                            nc.vector.tensor_copy(out=out_sb[:, :, hy, :, :], in_=src)
+                        else:
+                            nc.scalar.copy(out=out_sb[:, :, hy, :, :], in_=src)
+                    nc.sync.dma_start(
+                        out=out[b, :, i_first * HS : (i_first + I_STORE) * HS, :].rearrange("c y z -> c (y z)"),
+                        in_=out_sb[:].rearrange("p i h j w -> p (i h j w)"),
+                    )

@@ -20,9 +20,8 @@ CHUNK_COLS = I_CHUNK * I_STEP
 TAPS = K * K
 W_COLS = TAPS * C
 QUANT_MAX = 4096
-H_VECTOR = 3
-C_VECTOR_FIRST = 8
-C_VECTOR = 60
+H_VECTOR = 2
+C_VECTOR = 72
 I_STORE = 8
 
 FLOPS = 2 * HS * WS * N_PIX * O * W_COLS
@@ -31,7 +30,7 @@ BYTES = 2 * HS * WS * O * W_COLS + 2 * B * O * H * W + 4 * B * C * H * W
 
 def tile_patternconv_t_kernel(tc, x, weight, bias, grad_out, out):
     nc = tc.nc
-    with tc.tile_pool(name="keep", bufs=1) as keep, tc.tile_pool(name="w_raw", bufs=3) as w_raw_pool, tc.tile_pool(
+    with tc.tile_pool(name="keep", bufs=1) as keep, tc.tile_pool(name="w_raw", bufs=4) as w_raw_pool, tc.tile_pool(
         name="w_grouped", bufs=2
     ) as w_grouped_pool, tc.tile_pool(name="w_mx", bufs=8) as w_mx, tc.psum_pool(name="psum", bufs=8) as psum:
         g_codes = keep.tile([P, HS * WS, I_STEP + N_PIX], U32, align_bytes=64)
@@ -73,18 +72,17 @@ def tile_patternconv_t_kernel(tc, x, weight, bias, grad_out, out):
                 )
             quantised[(h_src, w_src)] = (w_codes, w_scales)
 
-        with tc.tile_pool(name="g_raw", bufs=2) as g_raw_pool, tc.tile_pool(name="g_grouped", bufs=2) as g_grouped_pool:
+        with tc.tile_pool(name="g_raw", bufs=6) as g_raw_pool, tc.tile_pool(name="g_grouped", bufs=2) as g_grouped_pool:
 
             def regroup_grad(m):
                 rows = slice(m * I_CHUNK * HS, (m + 1) * I_CHUNK * HS)
-                g_raw = g_raw_pool.tile([P, B, PACK, I_CHUNK * HS * W], BF16)
-                for b in range(B):
-                    nc.sync.dma_start(
-                        out=g_raw[:, b], in_=grad_out[b, :, rows, :].rearrange("(p t) y z -> p t (y z)", t=PACK)
-                    )
                 g_grouped = g_grouped_pool.tile([P, HS, WS, I_CHUNK, B, NJ, PACK], BF16, align_bytes=64)
                 for b in range(B):
-                    by_place = g_raw[:, b].rearrange("p t (i h j w) -> p h i j t w", i=I_CHUNK, h=HS, j=NJ, w=WS)
+                    g_raw = g_raw_pool.tile([P, PACK, I_CHUNK * HS * W], BF16)
+                    nc.sync.dma_start(
+                        out=g_raw[:], in_=grad_out[b, :, rows, :].rearrange("(p t) y z -> p t (y z)", t=PACK)
+                    )
+                    by_place = g_raw[:].rearrange("p t (i h j w) -> p h i j t w", i=I_CHUNK, h=HS, j=NJ, w=WS)
                     for h in range(HS):
                         dst = g_grouped[:, h, :, :, b, :, :].rearrange("p w i j t -> p i j t w")
                         if h < H_VECTOR:
@@ -104,14 +102,12 @@ def tile_patternconv_t_kernel(tc, x, weight, bias, grad_out, out):
                         in_=g_grouped[:, place // WS, place % WS].rearrange("p i b j t -> p (i b j t)"),
                     )
 
-            assert N_CHUNKS == HS
             grouped = {}
             for m in range(N_CHUNKS + 1):
                 if m < N_CHUNKS:
-                    grouped[m] = (regroup_grad(m), regroup_weights(m, 0, C_VECTOR_FIRST))
+                    grouped[m] = regroup_grad(m)
                 if m > 0:
-                    quantise_grad(m - 1, grouped[m - 1][0])
-                    quantise_weights(m - 1, 0, grouped[m - 1][1])
+                    quantise_grad(m - 1, grouped[m - 1])
             for low_place in range(2 * WS):
                 nc.vector.tensor_copy(
                     out=g_scales_down[:, low_place, I_STEP:N_PIX].bitcast(I32),
@@ -173,9 +169,7 @@ def tile_patternconv_t_kernel(tc, x, weight, bias, grad_out, out):
                     for h_again in range(HS):
                         add_passes(h_again, w_src, K - 1)
 
-            for h_src in range(HS):
-                multiply(h_src, 0)
-            places = [(h_src, w_src) for w_src in range(1, WS) for h_src in range(HS)]
+            places = [(h_src, w_src) for w_src in range(WS) for h_src in range(HS)]
             w_grouped_of = {}
             for n in range(len(places) + 1):
                 if n < len(places):

@@ -21,7 +21,8 @@ TAPS = K * K
 W_COLS = TAPS * C
 QUANT_MAX = 4096
 H_VECTOR = 2
-C_VECTOR = 72
+U_VECTOR = 2
+C_VECTOR = 108
 I_STORE = 8
 
 FLOPS = 2 * HS * WS * N_PIX * O * W_COLS
@@ -48,14 +49,15 @@ def tile_patternconv_t_kernel(tc, x, weight, bias, grad_out, out):
                 in_=weight[h_src, w_src].rearrange("(p t) c u v -> p (t c u v)", t=PACK),
             )
             w_grouped = w_grouped_pool.tile([P, K, K, C, PACK], BF16, align_bytes=64)
+            nc.vector.tensor_copy(
+                out=w_grouped[:, 0:U_VECTOR, :, 0:c_vector, :].rearrange("p u v c t -> p u c t v"),
+                in_=w_raw[:, :, 0:c_vector, 0:U_VECTOR, :].rearrange("p t c u v -> p u c t v"),
+            )
             for u in range(K):
-                nc.vector.tensor_copy(
-                    out=w_grouped[:, u, :, 0:c_vector, :].rearrange("p v c t -> p c t v"),
-                    in_=w_raw[:, :, 0:c_vector, u, :].rearrange("p t c v -> p c t v"),
-                )
+                c_first = c_vector if u < U_VECTOR else 0
                 nc.scalar.copy(
-                    out=w_grouped[:, u, :, c_vector:C, :].rearrange("p v c t -> p c t v"),
-                    in_=w_raw[:, :, c_vector:C, u, :].rearrange("p t c v -> p c t v"),
+                    out=w_grouped[:, u, :, c_first:C, :].rearrange("p v c t -> p c t v"),
+                    in_=w_raw[:, :, c_first:C, u, :].rearrange("p t c v -> p c t v"),
                 )
             return w_grouped
 

@@ -24,6 +24,7 @@ H_VECTOR = 2
 U_VECTOR = 2
 C_VECTOR = 108
 I_STORE = 8
+EARLY_PLACES = 2
 
 FLOPS = 2 * HS * WS * N_PIX * O * W_COLS
 BYTES = 2 * HS * WS * O * W_COLS + 2 * B * O * H * W + 4 * B * C * H * W
@@ -42,12 +43,22 @@ def tile_patternconv_t_kernel(tc, x, weight, bias, grad_out, out):
         nc.vector.memset(g_scales_down[:].bitcast(I32), 0)
         quantised = {}
 
-        def regroup_weights(h_src, w_src, c_vector):
+        places = [(h_src, w_src) for w_src in range(WS) for h_src in range(HS)]
+        loaded = []
+
+        def load_weights():
+            h_src, w_src = places[len(loaded)]
             w_raw = w_raw_pool.tile([P, PACK, C, K, K], BF16)
             nc.sync.dma_start(
                 out=w_raw[:].rearrange("p t c u v -> p (t c u v)"),
                 in_=weight[h_src, w_src].rearrange("(p t) c u v -> p (t c u v)", t=PACK),
             )
+            loaded.append(w_raw)
+
+        def regroup_weights(n, c_vector):
+            if len(loaded) == n:
+                load_weights()
+            w_raw = loaded[n]
             w_grouped = w_grouped_pool.tile([P, K, K, C, PACK], BF16, align_bytes=64)
             nc.vector.tensor_copy(
                 out=w_grouped[:, 0:U_VECTOR, :, 0:c_vector, :].rearrange("p u v c t -> p u c t v"),
@@ -107,6 +118,8 @@ def tile_patternconv_t_kernel(tc, x, weight, bias, grad_out, out):
             grouped = {}
             for m in range(N_CHUNKS + 1):
                 if m < N_CHUNKS:
+                    if m >= N_CHUNKS - EARLY_PLACES:
+                        load_weights()
                     grouped[m] = regroup_grad(m)
                 if m > 0:
                     quantise_grad(m - 1, grouped[m - 1])
@@ -171,11 +184,10 @@ def tile_patternconv_t_kernel(tc, x, weight, bias, grad_out, out):
                     for h_again in range(HS):
                         add_passes(h_again, w_src, K - 1)
 
-            places = [(h_src, w_src) for w_src in range(WS) for h_src in range(HS)]
             w_grouped_of = {}
             for n in range(len(places) + 1):
                 if n < len(places):
-                    w_grouped_of[n] = regroup_weights(places[n][0], places[n][1], C_VECTOR)
+                    w_grouped_of[n] = regroup_weights(n, C_VECTOR)
                 if n > 0:
                     quantise_weights(places[n - 1][0], places[n - 1][1], w_grouped_of[n - 1])
                     multiply(places[n - 1][0], places[n - 1][1])

@@ -67,8 +67,8 @@ def tile_patternconv_t_kernel(tc, x, weight, bias, grad_out, out):
             for u in range(K):
                 c_first = c_vector if u < U_VECTOR else 0
                 nc.scalar.copy(
-                    out=w_grouped[:, u, :, c_first:C, :].rearrange("p v c t -> p c t v"),
-                    in_=w_raw[:, :, c_first:C, u, :].rearrange("p t c v -> p c t v"),
+                    out=w_grouped[:, u, :, c_first:C, :].rearrange("p v (c e) t -> p c t e v", e=2),
+                    in_=w_raw[:, :, c_first:C, u, :].rearrange("p t (c e) v -> p c t e v", e=2),
                 )
             return w_grouped
 
@@ -102,7 +102,10 @@ def tile_patternconv_t_kernel(tc, x, weight, bias, grad_out, out):
                             nc.vector.tensor_copy(out=dst, in_=by_place[:, h])
                         else:
                             for i in range(I_CHUNK):
-                                nc.scalar.copy(out=dst[:, i], in_=by_place[:, h, i])
+                                nc.scalar.copy(
+                                    out=dst[:, i].rearrange("p (j e) t w -> p j t e w", e=2),
+                                    in_=by_place[:, h, i].rearrange("p (j e) t w -> p j t e w", e=2),
+                                )
                 return g_grouped
 
             def quantise_grad(m, g_grouped):

@@ -60,10 +60,11 @@ def tile_patternconv_t_kernel(tc, x, weight, bias, grad_out, out):
                 load_weights()
             w_raw = loaded[n]
             w_grouped = w_grouped_pool.tile([P, K, K, C, PACK], BF16, align_bytes=64)
-            nc.vector.tensor_copy(
-                out=w_grouped[:, 0:U_VECTOR, :, 0:c_vector, :].rearrange("p u v c t -> p u c t v"),
-                in_=w_raw[:, :, 0:c_vector, 0:U_VECTOR, :].rearrange("p t c u v -> p u c t v"),
-            )
+            for u in range(U_VECTOR):
+                nc.vector.tensor_copy(
+                    out=w_grouped[:, u, :, 0:c_vector, :].rearrange("p v (c e) t -> p c t e v", e=2),
+                    in_=w_raw[:, :, 0:c_vector, u, :].rearrange("p t (c e) v -> p c t e v", e=2),
+                )
             for u in range(K):
                 c_first = c_vector if u < U_VECTOR else 0
                 nc.scalar.copy(

@@ -22,9 +22,8 @@ W_COLS = TAPS * C
 QUANT_MAX = 4096
 H_VECTOR = 2
 U_VECTOR = 2
-C_VECTOR = 108
-I_STORE = 8
-EARLY_PLACES = 2
+C_VECTOR = (108, 108, 108, 108)
+I_STORE = NI // 2
 
 FLOPS = 2 * HS * WS * N_PIX * O * W_COLS
 BYTES = 2 * HS * WS * O * W_COLS + 2 * B * O * H * W + 4 * B * C * H * W
@@ -33,179 +32,234 @@ BYTES = 2 * HS * WS * O * W_COLS + 2 * B * O * H * W + 4 * B * C * H * W
 def tile_patternconv_t_kernel(tc, x, weight, bias, grad_out, out):
     nc = tc.nc
     with tc.tile_pool(name="keep", bufs=1) as keep, tc.tile_pool(name="w_raw", bufs=4) as w_raw_pool, tc.tile_pool(
-        name="w_grouped", bufs=2
-    ) as w_grouped_pool, tc.tile_pool(name="w_mx", bufs=8) as w_mx, tc.psum_pool(name="psum", bufs=8) as psum:
+        name="w_grouped", bufs=3
+    ) as w_grouped_pool, tc.tile_pool(name="w_mx", bufs=8) as w_mx, tc.psum_pool(name="psum", bufs=8) as psum, tc.manual_schedule():
         g_codes = keep.tile([P, HS * WS, I_STEP + N_PIX], U32, align_bytes=64)
         g_scales = keep.tile([P, HS * WS, N_PIX], U8, align_bytes=64)
         g_scales_down = keep.tile([P, 2 * WS, N_PIX], U8, align_bytes=64)
         nc.vector.memset(g_codes[:, :, 0:I_STEP].bitcast(I32), 0)
         nc.vector.memset(g_scales[:].bitcast(I32), 0)
         nc.vector.memset(g_scales_down[:].bitcast(I32), 0)
-        quantised = {}
 
-        places = [(h_src, w_src) for w_src in range(WS) for h_src in range(HS)]
-        loaded = []
+        places = [(h, w) for w in range(WS) for h in range(HS)]
+        last = len(places) - 1
+        w_raw_of = {}
+        w_grouped_of = {}
+        w_mx_of = {}
 
-        def load_weights():
-            h_src, w_src = places[len(loaded)]
+        def load_weights(n):
+            h, w = places[n]
             w_raw = w_raw_pool.tile([P, PACK, C, K, K], BF16)
             nc.sync.dma_start(
                 out=w_raw[:].rearrange("p t c u v -> p (t c u v)"),
-                in_=weight[h_src, w_src].rearrange("(p t) c u v -> p (t c u v)", t=PACK),
+                in_=weight[h, w].rearrange("(p t) c u v -> p (t c u v)", t=PACK),
             )
-            loaded.append(w_raw)
+            w_raw_of[n] = w_raw
 
-        def regroup_weights(n, c_vector):
-            if len(loaded) == n:
-                load_weights()
-            w_raw = loaded[n]
+        def regroup_weights(engine, n, u, channels):
+            out_view = w_grouped_of[n][:, u, :, channels, :].rearrange("p v (c e) t -> p c t e v", e=2)
+            in_view = w_raw_of[n][:, :, channels, u, :].rearrange("p t (c e) v -> p c t e v", e=2)
+            if engine == "vector":
+                nc.vector.tensor_copy(out=out_view, in_=in_view)
+            else:
+                nc.scalar.copy(out=out_view, in_=in_view)
+
+        def regroup_weights_vector(n):
             w_grouped = w_grouped_pool.tile([P, K, K, C, PACK], BF16, align_bytes=64)
+            w_grouped_of[n] = w_grouped
             for u in range(U_VECTOR):
-                nc.vector.tensor_copy(
-                    out=w_grouped[:, u, :, 0:c_vector, :].rearrange("p v (c e) t -> p c t e v", e=2),
-                    in_=w_raw[:, :, 0:c_vector, u, :].rearrange("p t (c e) v -> p c t e v", e=2),
-                )
-            for u in range(K):
-                c_first = c_vector if u < U_VECTOR else 0
-                nc.scalar.copy(
-                    out=w_grouped[:, u, :, c_first:C, :].rearrange("p v (c e) t -> p c t e v", e=2),
-                    in_=w_raw[:, :, c_first:C, u, :].rearrange("p t (c e) v -> p c t e v", e=2),
-                )
-            return w_grouped
+                regroup_weights("vector", n, u, slice(0, C_VECTOR[places[n][1]]))
 
-        def quantise_weights(h_src, w_src, w_grouped):
+        def quantise_weights(n):
             w_codes = w_mx.tile([P, W_COLS], U32, align_bytes=64)
             w_scales = w_mx.tile([P, W_COLS], U8, align_bytes=64)
-            flat = w_grouped[:].rearrange("p u v c t -> p (u v c t)")
-            for first in (0, QUANT_MAX // PACK):
-                last = min(first + QUANT_MAX // PACK, W_COLS)
+            flat = w_grouped_of[n][:].rearrange("p u v c t -> p (u v c t)")
+            for first in range(0, W_COLS, QUANT_MAX // PACK):
+                end = min(first + QUANT_MAX // PACK, W_COLS)
                 nc.vector.quantize_mx(
-                    out=w_codes[:, first:last].bitcast(E4M3X4),
-                    scales=w_scales[:, first:last],
-                    in_=flat[:, first * PACK : last * PACK],
+                    out=w_codes[:, first:end].bitcast(E4M3X4),
+                    scales=w_scales[:, first:end],
+                    in_=flat[:, first * PACK : end * PACK],
                 )
-            quantised[(h_src, w_src)] = (w_codes, w_scales)
+            w_mx_of[places[n]] = (w_codes, w_scales)
 
-        with tc.tile_pool(name="g_raw", bufs=6) as g_raw_pool, tc.tile_pool(name="g_grouped", bufs=2) as g_grouped_pool:
+        with tc.tile_pool(name="g_raw", bufs=5) as g_raw_pool, tc.tile_pool(name="g_grouped", bufs=2) as g_grouped_pool:
+            g_raw_of = {}
+            g_grouped_of = {}
 
-            def regroup_grad(m):
+            def load_grad(m, b):
                 rows = slice(m * I_CHUNK * HS, (m + 1) * I_CHUNK * HS)
-                g_grouped = g_grouped_pool.tile([P, HS, WS, I_CHUNK, B, NJ, PACK], BF16, align_bytes=64)
-                for b in range(B):
-                    g_raw = g_raw_pool.tile([P, PACK, I_CHUNK * HS * W], BF16)
-                    nc.sync.dma_start(
-                        out=g_raw[:], in_=grad_out[b, :, rows, :].rearrange("(p t) y z -> p t (y z)", t=PACK)
-                    )
-                    by_place = g_raw[:].rearrange("p t (i h j w) -> p h i j t w", i=I_CHUNK, h=HS, j=NJ, w=WS)
-                    for h in range(HS):
-                        dst = g_grouped[:, h, :, :, b, :, :].rearrange("p w i j t -> p i j t w")
-                        if h < H_VECTOR:
-                            nc.vector.tensor_copy(out=dst, in_=by_place[:, h])
-                        else:
-                            for i in range(I_CHUNK):
-                                nc.scalar.copy(
-                                    out=dst[:, i].rearrange("p (j e) t w -> p j t e w", e=2),
-                                    in_=by_place[:, h, i].rearrange("p (j e) t w -> p j t e w", e=2),
-                                )
-                return g_grouped
+                g_raw = g_raw_pool.tile([P, PACK, I_CHUNK * HS * W], BF16)
+                nc.sync.dma_start(
+                    out=g_raw[:], in_=grad_out[b, :, rows, :].rearrange("(p t) y z -> p t (y z)", t=PACK)
+                )
+                g_raw_of[(m, b)] = g_raw
 
-            def quantise_grad(m, g_grouped):
-                for place in range(HS * WS):
-                    cols = slice(m * CHUNK_COLS, (m + 1) * CHUNK_COLS)
-                    padded_cols = slice(I_STEP + m * CHUNK_COLS, I_STEP + (m + 1) * CHUNK_COLS)
+            def regroup_grad(m, b):
+                if b == 0:
+                    g_grouped = g_grouped_pool.tile([P, HS, WS, I_CHUNK, B, NJ, PACK], BF16, align_bytes=64)
+                    g_grouped_of[m] = g_grouped
+                by_place = g_raw_of[(m, b)][:].rearrange("p t (i h j w) -> p h i j t w", i=I_CHUNK, h=HS, j=NJ, w=WS)
+                for h in range(HS):
+                    dst = g_grouped_of[m][:, h, :, :, b, :, :].rearrange("p w i j t -> p i j t w")
+                    if h < H_VECTOR:
+                        nc.vector.tensor_copy(out=dst, in_=by_place[:, h])
+                    else:
+                        for i in range(I_CHUNK):
+                            nc.scalar.copy(
+                                out=dst[:, i].rearrange("p (j e) t w -> p j t e w", e=2),
+                                in_=by_place[:, h, i].rearrange("p (j e) t w -> p j t e w", e=2),
+                            )
+
+            def quantise_grad(m, places_of_part):
+                cols = slice(m * CHUNK_COLS, (m + 1) * CHUNK_COLS)
+                padded_cols = slice(I_STEP + m * CHUNK_COLS, I_STEP + (m + 1) * CHUNK_COLS)
+                for place in places_of_part:
                     nc.vector.quantize_mx(
                         out=g_codes[:, place, padded_cols].bitcast(E5M2X4),
                         scales=g_scales[:, place, cols],
-                        in_=g_grouped[:, place // WS, place % WS].rearrange("p i b j t -> p (i b j t)"),
+                        in_=g_grouped_of[m][:, place // WS, place % WS].rearrange("p i b j t -> p (i b j t)"),
                     )
 
-            grouped = {}
-            for m in range(N_CHUNKS + 1):
-                if m < N_CHUNKS:
-                    if m >= N_CHUNKS - EARLY_PLACES:
-                        load_weights()
-                    grouped[m] = regroup_grad(m)
-                if m > 0:
-                    quantise_grad(m - 1, grouped[m - 1])
-            for low_place in range(2 * WS):
-                nc.vector.tensor_copy(
-                    out=g_scales_down[:, low_place, I_STEP:N_PIX].bitcast(I32),
-                    in_=g_scales[:, 2 * WS + low_place, 0 : N_PIX - I_STEP].bitcast(I32),
-                )
+            halves = (range(0, HS * WS // 2), range(HS * WS // 2, HS * WS))
+            for m in range(N_CHUNKS):
+                for b in range(B):
+                    load_grad(m, b)
+                    regroup_grad(m, b)
+                    if m > 0:
+                        quantise_grad(m - 1, halves[b])
+            for n in range(3):
+                load_weights(n)
+            regroup_weights_vector(0)
+            for u in range(K):
+                regroup_weights("scalar", 0, u, slice(C_VECTOR[0] if u < U_VECTOR else 0, C))
+            for half in halves:
+                quantise_grad(N_CHUNKS - 1, half)
+            nc.vector.tensor_copy(
+                out=g_scales_down[:, :, I_STEP:N_PIX].bitcast(I32),
+                in_=g_scales[:, 2 * WS :, 0 : N_PIX - I_STEP].bitcast(I32),
+            )
 
-        with tc.tile_pool(name="planes", bufs=1) as planes_pool, tc.tile_pool(name="out_sb", bufs=4) as out_pool:
+        with tc.tile_pool(name="planes", bufs=1) as planes_pool, tc.tile_pool(name="out_sb", bufs=1) as out_pool:
             planes = planes_pool.tile([P, HS, WS, NI, B, NJ], F32)
-            open_groups = {}
+            out_sb = out_pool.tile([P, NI // I_STORE, B, I_STORE, HS, NJ, WS], F32)
+            whole = (0, NI)
+            pieces = [(i_first, i_first + I_STORE) for i_first in range(0, NI, I_STORE)]
+            acc_of = {}
             passes_done = {}
 
-            def close_group(hy, wz, dj, acc):
-                plane = planes[:, hy, wz]
+            def close(key, i_range=whole):
+                hy, wz, dj = key
+                i0, i1 = i_range
+                plane = planes[:, hy, wz, i0:i1]
+                acc = acc_of[key][:, i0 * I_STEP : i1 * I_STEP]
                 if dj == 0:
-                    nc.scalar.copy(out=plane.rearrange("p i b j -> p (i b j)"), in_=acc[:])
+                    nc.scalar.copy(out=plane.rearrange("p i b j -> p (i b j)"), in_=acc)
                 else:
-                    shifted = acc[:].rearrange("p (i b j) -> p i b j", i=NI, b=B)
+                    shifted = acc.rearrange("p (i b j) -> p i b j", i=i1 - i0, b=B)
                     nc.vector.tensor_add(
                         out=plane[:, :, :, 1:NJ], in0=shifted[:, :, :, 0 : NJ - 1], in1=plane[:, :, :, 1:NJ]
                     )
 
-            def add_passes(h_src, w_src, v):
-                w_codes, w_scales = quantised[(h_src, w_src)]
-                wz, dj = (w_src + v) % WS, (w_src + v) // WS
+            def run_pass(h, w, u, v):
+                w_codes, w_scales = w_mx_of[(h, w)]
+                hy, di = (h + u) % HS, (h + u) // HS
+                wz, dj = (w + v) % WS, (w + v) // WS
+                key = (hy, wz, dj)
                 source_columns = min(wz + 1, K) if dj == 0 else K - 1 - wz
+                if key not in acc_of:
+                    acc = psum.tile([P, N_PIX], F32)
+                    acc_of[key] = acc
+                    passes_done[key] = 0
+                place = h * WS + w
+                if di == 0:
+                    rhs = g_codes[:, place, I_STEP : I_STEP + N_PIX]
+                    rhs_scale = g_scales[:, place, :]
+                else:
+                    rhs = g_codes[:, place, 0:N_PIX]
+                    rhs_scale = g_scales_down[:, place - 2 * WS, :]
+                tap = slice((u * K + v) * C, (u * K + v + 1) * C)
+                passes_done[key] += 1
+                full = passes_done[key] == K * source_columns
+                nc.tensor.matmul_mx(
+                    out=acc_of[key][:],
+                    lhsT=w_codes[:, tap].bitcast(E4M3X4),
+                    lhsT_scale=w_scales[:, tap],
+                    rhs=rhs.bitcast(E5M2X4),
+                    rhs_scale=rhs_scale,
+                    start=(passes_done[key] == 1),
+                    stop=full,
+                )
+                return [key] if full else []
+
+            def run_passes(passes):
+                return [key for one in passes for key in run_pass(*one)]
+
+            def direct_passes(n):
+                h, w = places[n]
+                return [(h, w, u, v) for u in ((0, 1, 2) if h == 2 else range(K)) for v in range(K - 1)]
+
+            def held_passes(w, hy):
+                return [(h, w, (hy - h) % HS, K - 1) for h in range(HS) if (hy - h) % HS < K]
+
+            held_rows = {2: (2,), 3: (3, 0, 1)}
+            finished = []
+            for n in range(1, last + 1):
+                if n + 2 <= last:
+                    load_weights(n + 2)
+                regroup_weights_vector(n)
+                regroup_weights("scalar", n, U_VECTOR, slice(0, C))
+                for key in finished:
+                    close(key)
+                if n > 1:
+                    h, w = places[n - 2]
+                    for hy in held_rows.get(h, ()):
+                        run_passes(held_passes(w, hy))
+                for u in range(U_VECTOR):
+                    regroup_weights("scalar", n, u, slice(C_VECTOR[places[n][1]], C))
+                quantise_weights(n - 1)
+                finished = run_passes(direct_passes(n - 1))
+
+            w = WS - 1
+            quantise_weights(last)
+            for key in finished:
+                close(key)
+            for key in run_passes(held_passes(w, 2)):
+                close(key)
+
+            def lay_out(engine, piece, b, hy):
+                i0, i1 = pieces[piece]
+                src = planes[:, hy, :, i0:i1, b, :].rearrange("p w i j -> p i j w")
+                dst = out_sb[:, piece, b, :, hy, :, :]
+                if engine == "vector":
+                    nc.vector.tensor_copy(out=dst, in_=src)
+                else:
+                    nc.scalar.copy(out=dst, in_=src)
+
+            last_rows = (3, 0, 1)
+            for v in (1, 0):
                 for u in range(K):
-                    hy, di = (h_src + u) % HS, (h_src + u) // HS
-                    key = (hy, wz, dj)
-                    if key not in open_groups:
-                        acc = psum.tile([P, N_PIX], F32)
-                        open_groups[key] = acc
-                        passes_done[key] = 0
-                    acc = open_groups[key]
-                    place = h_src * WS + w_src
-                    if di == 0:
-                        rhs = g_codes[:, place, I_STEP : I_STEP + N_PIX]
-                        rhs_scale = g_scales[:, place, :]
+                    for key in run_pass(HS - 1, w, u, v):
+                        close(key)
+            for piece in range(len(pieces)):
+                for b in range(B):
+                    lay_out("scalar", piece, b, 2)
+            final_keys = []
+            for hy in last_rows:
+                for key in run_passes(held_passes(w, hy)):
+                    if hy == 3:
+                        close(key)
                     else:
-                        rhs = g_codes[:, place, 0:N_PIX]
-                        rhs_scale = g_scales_down[:, place - 2 * WS, :]
-                    tap = slice((u * K + v) * C, (u * K + v + 1) * C)
-                    passes_done[key] += 1
-                    nc.tensor.matmul_mx(
-                        out=acc[:],
-                        lhsT=w_codes[:, tap].bitcast(E4M3X4),
-                        lhsT_scale=w_scales[:, tap],
-                        rhs=rhs.bitcast(E5M2X4),
-                        rhs_scale=rhs_scale,
-                        start=(passes_done[key] == 1),
-                        stop=(passes_done[key] == K * source_columns),
-                    )
-                    if passes_done[key] == K * source_columns:
-                        close_group(hy, wz, dj, acc)
-
-            def multiply(h_src, w_src):
-                for v in range(K - 1):
-                    add_passes(h_src, w_src, v)
-                if h_src == HS - 1:
-                    for h_again in range(HS):
-                        add_passes(h_again, w_src, K - 1)
-
-            w_grouped_of = {}
-            for n in range(len(places) + 1):
-                if n < len(places):
-                    w_grouped_of[n] = regroup_weights(n, C_VECTOR)
-                if n > 0:
-                    quantise_weights(places[n - 1][0], places[n - 1][1], w_grouped_of[n - 1])
-                    multiply(places[n - 1][0], places[n - 1][1])
-
-            for b in range(B):
-                for i_first in range(0, NI, I_STORE):
-                    out_sb = out_pool.tile([P, I_STORE, HS, NJ, WS], F32)
-                    for hy in range(HS):
-                        src = planes[:, hy, :, i_first : i_first + I_STORE, b, :].rearrange("p w i j -> p i j w")
-                        if hy < HS - 1:
-                            nc.vector.tensor_copy(out=out_sb[:, :, hy, :, :], in_=src)
-                        else:
-                            nc.scalar.copy(out=out_sb[:, :, hy, :, :], in_=src)
+                        final_keys.append(key)
+            for piece, i_range in enumerate(pieces):
+                for key in final_keys:
+                    close(key, i_range)
+                for b in range(B):
+                    lay_out("scalar", piece, b, 3)
+                    lay_out("vector", piece, b, 0)
+                    lay_out("vector", piece, b, 1)
+                    i0, i1 = i_range
                     nc.sync.dma_start(
-                        out=out[b, :, i_first * HS : (i_first + I_STORE) * HS, :].rearrange("c y z -> c (y z)"),
-                        in_=out_sb[:].rearrange("p i h j w -> p (i h j w)"),
+                        out=out[b, :, i0 * HS : i1 * HS, :].rearrange("c y z -> c (y z)"),
+                        in_=out_sb[:, piece, b].rearrange("p i h j w -> p (i h j w)"),
                     )

@@ -20,9 +20,10 @@ CHUNK_COLS = I_CHUNK * I_STEP
 TAPS = K * K
 W_COLS = TAPS * C
 QUANT_MAX = 4096
-H_VECTOR = 2
-U_VECTOR = 2
-C_VECTOR = (108, 108, 108, 108)
+H_VECTOR = (2, 2, 2, 2)
+C_FULL = 76
+C_A = 88
+C_B = 88
 I_STORE = NI // 2
 
 FLOPS = 2 * HS * WS * N_PIX * O * W_COLS
@@ -33,59 +34,121 @@ def tile_patternconv_t_kernel(tc, x, weight, bias, grad_out, out):
     nc = tc.nc
     with tc.tile_pool(name="keep", bufs=1) as keep, tc.tile_pool(name="w_raw", bufs=4) as w_raw_pool, tc.tile_pool(
         name="w_grouped", bufs=3
-    ) as w_grouped_pool, tc.tile_pool(name="w_mx", bufs=8) as w_mx, tc.psum_pool(name="psum", bufs=8) as psum, tc.manual_schedule():
+    ) as w_grouped_pool, tc.tile_pool(name="w_mx", bufs=6) as w_mx, tc.tile_pool(
+        name="staging", bufs=2
+    ) as staging_pool, tc.psum_pool(name="psum", bufs=8) as psum, tc.manual_schedule():
         g_codes = keep.tile([P, HS * WS, I_STEP + N_PIX], U32, align_bytes=64)
         g_scales = keep.tile([P, HS * WS, N_PIX], U8, align_bytes=64)
         g_scales_down = keep.tile([P, 2 * WS, N_PIX], U8, align_bytes=64)
         nc.vector.memset(g_codes[:, :, 0:I_STEP].bitcast(I32), 0)
-        nc.vector.memset(g_scales[:].bitcast(I32), 0)
-        nc.vector.memset(g_scales_down[:].bitcast(I32), 0)
+        nc.vector.memset(g_scales[:, 2 * WS :].bitcast(I32), 0)
+        nc.vector.memset(g_scales_down[:, :, 0:I_STEP].bitcast(I32), 0)
 
         places = [(h, w) for w in range(WS) for h in range(HS)]
-        last = len(places) - 1
+        jobs = []
+        for w in range(WS):
+            if w not in ():
+                jobs += [(h, w, 0, K) for h in range(HS)]
+            else:
+                jobs += [(h, w, 0, K - 1) for h in range(HS)] + [(h, w, K - 1, K) for h in range(HS)]
         w_raw_of = {}
-        w_grouped_of = {}
+        grouped_of = {}
         w_mx_of = {}
+        quantised = set()
 
-        def load_weights(n):
+        def load_weights(n, parts=1):
             h, w = places[n]
             w_raw = w_raw_pool.tile([P, PACK, C, K, K], BF16)
-            nc.sync.dma_start(
-                out=w_raw[:].rearrange("p t c u v -> p (t c u v)"),
-                in_=weight[h, w].rearrange("(p t) c u v -> p (t c u v)", t=PACK),
-            )
-            w_raw_of[n] = w_raw
+            for part in range(parts):
+                channels = slice(part * C // parts, (part + 1) * C // parts)
+                nc.sync.dma_start(
+                    out=w_raw[:, :, channels].rearrange("p t c u v -> p t (c u v)"),
+                    in_=weight[h, w, :, channels].rearrange("(p t) c u v -> p t (c u v)", t=PACK),
+                )
+            w_raw_of[(h, w)] = w_raw
 
-        def regroup_weights(engine, n, u, channels):
-            out_view = w_grouped_of[n][:, u, :, channels, :].rearrange("p v (c e) t -> p c t e v", e=2)
-            in_view = w_raw_of[n][:, :, channels, u, :].rearrange("p t (c e) v -> p c t e v", e=2)
+        def load_up_to(n):
+            while len(w_raw_of) <= min(n, len(places) - 1):
+                load_weights(len(w_raw_of))
+
+        def regroup(engine, job, u, channels):
+            h, w, v0, v1 = job
+            run = 2 if v1 - v0 == K else 4
+            out_view = grouped_of[job][:, :, u, channels, :].rearrange("p v (c e) t -> p c t e v", e=run)
+            in_view = w_raw_of[(h, w)][:, :, channels, u, v0:v1].rearrange("p t (c e) v -> p c t e v", e=run)
             if engine == "vector":
                 nc.vector.tensor_copy(out=out_view, in_=in_view)
             else:
                 nc.scalar.copy(out=out_view, in_=in_view)
 
-        def regroup_weights_vector(n):
-            w_grouped = w_grouped_pool.tile([P, K, K, C, PACK], BF16, align_bytes=64)
-            w_grouped_of[n] = w_grouped
-            for u in range(U_VECTOR):
-                regroup_weights("vector", n, u, slice(0, C_VECTOR[places[n][1]]))
+        def grouped_tile(job):
+            if job not in grouped_of:
+                w_grouped = w_grouped_pool.tile([P, job[3] - job[2], K, C, PACK], BF16, align_bytes=64)
+                grouped_of[job] = w_grouped
 
-        def quantise_weights(n):
-            w_codes = w_mx.tile([P, W_COLS], U32, align_bytes=64)
-            w_scales = w_mx.tile([P, W_COLS], U8, align_bytes=64)
-            flat = w_grouped_of[n][:].rearrange("p u v c t -> p (u v c t)")
-            for first in range(0, W_COLS, QUANT_MAX // PACK):
-                end = min(first + QUANT_MAX // PACK, W_COLS)
+        def share(job):
+            return {K: C_FULL, K - 1: C_A, 1: C_B}[job[3] - job[2]]
+
+        def regroup_vector(job):
+            grouped_tile(job)
+            regroup("vector", job, 0, slice(0, C))
+            if share(job) > 0:
+                regroup("vector", job, 1, slice(0, share(job)))
+
+        def regroup_whole(n, c0, c1):
+            job = jobs[n]
+            grouped_tile(job)
+            cm = c0 + (c1 - c0) * C_FULL // C // 2 * 2
+            regroup("vector", job, 0, slice(c0, c1))
+            regroup("vector", job, 1, slice(c0, cm))
+            regroup("scalar", job, 1, slice(cm, c1))
+            regroup("scalar", job, 2, slice(c0, c1))
+
+        def quantise_job(job):
+            if job in quantised:
+                return
+            quantised.add(job)
+            h, w, v0, v1 = job
+            columns = (v1 - v0) * K * C
+            w_codes = w_mx.tile([P, columns], U32, align_bytes=64)
+            w_scales = w_mx.tile([P, columns], U8, align_bytes=64)
+            flat = grouped_of[job][:].rearrange("p v u c t -> p (v u c t)")
+            first = 0
+            while first < columns:
+                width = QUANT_MAX // PACK
+                while width > columns - first:
+                    width = width // 2
                 nc.vector.quantize_mx(
-                    out=w_codes[:, first:end].bitcast(E4M3X4),
-                    scales=w_scales[:, first:end],
-                    in_=flat[:, first * PACK : end * PACK],
+                    out=w_codes[:, first : first + width].bitcast(E4M3X4),
+                    scales=w_scales[:, first : first + width],
+                    in_=flat[:, first * PACK : (first + width) * PACK],
                 )
-            w_mx_of[places[n]] = (w_codes, w_scales)
+                first += width
+            for v in range(v0, v1):
+                for u in range(K):
+                    tap = slice(((v - v0) * K + u) * C, ((v - v0) * K + u + 1) * C)
+                    w_mx_of[(h, w, u, v)] = (w_codes[:, tap], w_scales[:, tap])
 
-        with tc.tile_pool(name="g_raw", bufs=5) as g_raw_pool, tc.tile_pool(name="g_grouped", bufs=2) as g_grouped_pool:
-            g_raw_of = {}
-            g_grouped_of = {}
+        g_raw_of = {}
+        g_grouped_of = {}
+
+        def quantise_grad(m, w):
+            cols = slice(m * CHUNK_COLS, (m + 1) * CHUNK_COLS)
+            padded_cols = slice(I_STEP + m * CHUNK_COLS, I_STEP + (m + 1) * CHUNK_COLS)
+            for h in range(HS):
+                nc.vector.quantize_mx(
+                    out=g_codes[:, h * WS + w, padded_cols].bitcast(E5M2X4),
+                    scales=g_scales[:, h * WS + w, cols],
+                    in_=g_grouped_of[m][:, h, w].rearrange("p i b j t -> p (i b j t)"),
+                )
+
+        def copy_scales_down(w):
+            nc.vector.tensor_copy(
+                out=g_scales_down[:, w::WS, I_STEP:N_PIX].bitcast(I32),
+                in_=g_scales[:, 2 * WS + w :: WS, 0 : N_PIX - I_STEP].bitcast(I32),
+            )
+
+        with tc.tile_pool(name="g_raw", bufs=5) as g_raw_pool:
 
             def load_grad(m, b):
                 rows = slice(m * I_CHUNK * HS, (m + 1) * I_CHUNK * HS)
@@ -97,12 +160,12 @@ def tile_patternconv_t_kernel(tc, x, weight, bias, grad_out, out):
 
             def regroup_grad(m, b):
                 if b == 0:
-                    g_grouped = g_grouped_pool.tile([P, HS, WS, I_CHUNK, B, NJ, PACK], BF16, align_bytes=64)
+                    g_grouped = staging_pool.tile([P, HS, WS, I_CHUNK, B, NJ, PACK], BF16, align_bytes=64, name="staging")
                     g_grouped_of[m] = g_grouped
                 by_place = g_raw_of[(m, b)][:].rearrange("p t (i h j w) -> p h i j t w", i=I_CHUNK, h=HS, j=NJ, w=WS)
                 for h in range(HS):
                     dst = g_grouped_of[m][:, h, :, :, b, :, :].rearrange("p w i j t -> p i j t w")
-                    if h < H_VECTOR:
+                    if h < H_VECTOR[m]:
                         nc.vector.tensor_copy(out=dst, in_=by_place[:, h])
                     else:
                         for i in range(I_CHUNK):
@@ -111,38 +174,49 @@ def tile_patternconv_t_kernel(tc, x, weight, bias, grad_out, out):
                                 in_=by_place[:, h, i].rearrange("p (j e) t w -> p j t e w", e=2),
                             )
 
-            def quantise_grad(m, places_of_part):
-                cols = slice(m * CHUNK_COLS, (m + 1) * CHUNK_COLS)
-                padded_cols = slice(I_STEP + m * CHUNK_COLS, I_STEP + (m + 1) * CHUNK_COLS)
-                for place in places_of_part:
-                    nc.vector.quantize_mx(
-                        out=g_codes[:, place, padded_cols].bitcast(E5M2X4),
-                        scales=g_scales[:, place, cols],
-                        in_=g_grouped_of[m][:, place // WS, place % WS].rearrange("p i b j t -> p (i b j t)"),
-                    )
+            load_weights(0, 2)
+            load_weights(1, 2)
+            load_grad(0, 0)
+            load_grad(0, 1)
+            load_grad(1, 0)
+            regroup_whole(0, 0, C // 2)
+            regroup_whole(0, C // 2, C)
+            regroup_whole(1, 0, C // 2)
+            quantise_job(jobs[0])
+            regroup_whole(1, C // 2, C)
+            regroup_grad(0, 0)
+            quantise_job(jobs[1])
+            regroup_grad(0, 1)
+            load_grad(1, 1)
+            regroup_grad(1, 0)
+            quantise_grad(0, 0)
+            quantise_grad(0, 1)
+            regroup_grad(1, 1)
+            quantise_grad(0, 2)
+            quantise_grad(0, 3)
+            load_grad(2, 0)
+            regroup_grad(2, 0)
+            quantise_grad(1, 0)
+            quantise_grad(1, 1)
+            load_grad(2, 1)
+            regroup_grad(2, 1)
+            quantise_grad(1, 2)
+            quantise_grad(1, 3)
+            load_grad(3, 0)
+            regroup_grad(3, 0)
+            quantise_grad(2, 0)
+            quantise_grad(2, 1)
+            load_grad(3, 1)
+            regroup_grad(3, 1)
+            quantise_grad(2, 2)
+            quantise_grad(2, 3)
+            load_weights(2, 1)
+            load_weights(3, 1)
+            quantise_grad(3, 0)
+            copy_scales_down(0)
 
-            halves = (range(0, HS * WS // 2), range(HS * WS // 2, HS * WS))
-            for m in range(N_CHUNKS):
-                for b in range(B):
-                    load_grad(m, b)
-                    regroup_grad(m, b)
-                    if m > 0:
-                        quantise_grad(m - 1, halves[b])
-            for n in range(3):
-                load_weights(n)
-            regroup_weights_vector(0)
-            for u in range(K):
-                regroup_weights("scalar", 0, u, slice(C_VECTOR[0] if u < U_VECTOR else 0, C))
-            for half in halves:
-                quantise_grad(N_CHUNKS - 1, half)
-            nc.vector.tensor_copy(
-                out=g_scales_down[:, :, I_STEP:N_PIX].bitcast(I32),
-                in_=g_scales[:, 2 * WS :, 0 : N_PIX - I_STEP].bitcast(I32),
-            )
-
-        with tc.tile_pool(name="planes", bufs=1) as planes_pool, tc.tile_pool(name="out_sb", bufs=1) as out_pool:
+        with tc.tile_pool(name="planes", bufs=1) as planes_pool:
             planes = planes_pool.tile([P, HS, WS, NI, B, NJ], F32)
-            out_sb = out_pool.tile([P, NI // I_STORE, B, I_STORE, HS, NJ, WS], F32)
             whole = (0, NI)
             pieces = [(i_first, i_first + I_STORE) for i_first in range(0, NI, I_STORE)]
             acc_of = {}
@@ -162,7 +236,7 @@ def tile_patternconv_t_kernel(tc, x, weight, bias, grad_out, out):
                     )
 
             def run_pass(h, w, u, v):
-                w_codes, w_scales = w_mx_of[(h, w)]
+                w_codes, w_scales = w_mx_of[(h, w, u, v)]
                 hy, di = (h + u) % HS, (h + u) // HS
                 wz, dj = (w + v) % WS, (w + v) // WS
                 key = (hy, wz, dj)
@@ -178,13 +252,12 @@ def tile_patternconv_t_kernel(tc, x, weight, bias, grad_out, out):
                 else:
                     rhs = g_codes[:, place, 0:N_PIX]
                     rhs_scale = g_scales_down[:, place - 2 * WS, :]
-                tap = slice((u * K + v) * C, (u * K + v + 1) * C)
                 passes_done[key] += 1
                 full = passes_done[key] == K * source_columns
                 nc.tensor.matmul_mx(
                     out=acc_of[key][:],
-                    lhsT=w_codes[:, tap].bitcast(E4M3X4),
-                    lhsT_scale=w_scales[:, tap],
+                    lhsT=w_codes.bitcast(E4M3X4),
+                    lhsT_scale=w_scales,
                     rhs=rhs.bitcast(E5M2X4),
                     rhs_scale=rhs_scale,
                     start=(passes_done[key] == 1),
@@ -195,71 +268,99 @@ def tile_patternconv_t_kernel(tc, x, weight, bias, grad_out, out):
             def run_passes(passes):
                 return [key for one in passes for key in run_pass(*one)]
 
-            def direct_passes(n):
-                h, w = places[n]
-                return [(h, w, u, v) for u in ((0, 1, 2) if h == 2 else range(K)) for v in range(K - 1)]
-
             def held_passes(w, hy):
                 return [(h, w, (hy - h) % HS, K - 1) for h in range(HS) if (hy - h) % HS < K]
 
             held_rows = {2: (2,), 3: (3, 0, 1)}
-            finished = []
-            for n in range(1, last + 1):
-                if n + 2 <= last:
-                    load_weights(n + 2)
-                regroup_weights_vector(n)
-                regroup_weights("scalar", n, U_VECTOR, slice(0, C))
-                for key in finished:
-                    close(key)
-                if n > 1:
-                    h, w = places[n - 2]
+
+            def multiply(job):
+                h, w, v0, v1 = job
+                taps = range(v0, v1) if v1 - v0 < K else range(v0, K - 1)
+                return run_passes([(h, w, u, v) for v in taps for u in range(K)])
+
+            def multiply_held(job):
+                h, w, v0, v1 = job
+                keys = []
+                if v1 - v0 == K:
                     for hy in held_rows.get(h, ()):
-                        run_passes(held_passes(w, hy))
-                for u in range(U_VECTOR):
-                    regroup_weights("scalar", n, u, slice(C_VECTOR[places[n][1]], C))
-                quantise_weights(n - 1)
-                finished = run_passes(direct_passes(n - 1))
+                        keys += run_passes(held_passes(w, hy))
+                return keys
 
-            w = WS - 1
-            quantise_weights(last)
-            for key in finished:
-                close(key)
-            for key in run_passes(held_passes(w, 2)):
-                close(key)
+            staged = []
 
-            def lay_out(engine, piece, b, hy):
-                i0, i1 = pieces[piece]
+            def lay_out(engine, b, hy, i0, i1):
                 src = planes[:, hy, :, i0:i1, b, :].rearrange("p w i j -> p i j w")
-                dst = out_sb[:, piece, b, :, hy, :, :]
+                dst = staged[b][:, i0:i1, hy, :, :]
                 if engine == "vector":
                     nc.vector.tensor_copy(out=dst, in_=src)
                 else:
                     nc.scalar.copy(out=dst, in_=src)
 
-            last_rows = (3, 0, 1)
-            for v in (1, 0):
-                for u in range(K):
-                    for key in run_pass(HS - 1, w, u, v):
-                        close(key)
-            for piece in range(len(pieces)):
-                for b in range(B):
-                    lay_out("scalar", piece, b, 2)
-            final_keys = []
-            for hy in last_rows:
-                for key in run_passes(held_passes(w, hy)):
-                    if hy == 3:
-                        close(key)
-                    else:
-                        final_keys.append(key)
-            for piece, i_range in enumerate(pieces):
-                for key in final_keys:
+            def late_work(n):
+                if n == 4:
+                    quantise_grad(3, 1)
+                    copy_scales_down(1)
+                if n == 8:
+                    quantise_grad(3, 2)
+                    copy_scales_down(2)
+                if n == 12:
+                    quantise_grad(3, 3)
+                    copy_scales_down(3)
+
+            finished = []
+            first = 2
+            for n in range(first - 1):
+                finished += multiply(jobs[n])
+            for n in range(first, len(jobs)):
+                job = jobs[n]
+                load_up_to(places.index(job[:2]) + 2)
+                regroup_vector(job)
+                regroup("scalar", job, 2, slice(0, C))
+                for key in finished:
+                    close(key)
+                if n > 1:
+                    multiply_held(jobs[n - 2])
+                if share(job) < C:
+                    regroup("scalar", job, 1, slice(share(job), C))
+                quantise_job(jobs[n - 1])
+                late_work(n)
+                finished = multiply(jobs[n - 1])
+            for b in range(B):
+                out_sb = staging_pool.tile([P, NI, HS, NJ, WS], F32, align_bytes=64, name="staging")
+                staged.append(out_sb)
+            quantise_job(jobs[-1])
+            for key in finished:
+                close(key)
+            for key in run_passes(held_passes(WS - 1, 2)):
+                close(key)
+            direct = multiply(jobs[-1])
+            for b in range(B):
+                lay_out("scalar", b, 2, 0, NI)
+                nc.sync.dma_start(
+                    out=out[b].rearrange("c (i h) z -> c i h z", h=HS)[:, :, 2, :],
+                    in_=staged[b][:, :, 2].rearrange("p i j w -> p i (j w)"),
+                )
+            for key in direct:
+                close(key)
+            last_keys = run_passes([q for hy in (3, 0, 1) for q in held_passes(WS - 1, hy)])
+            for half, i_range in enumerate(pieces):
+                for key in last_keys:
                     close(key, i_range)
+                i0, i1 = i_range
                 for b in range(B):
-                    lay_out("scalar", piece, b, 3)
-                    lay_out("vector", piece, b, 0)
-                    lay_out("vector", piece, b, 1)
-                    i0, i1 = i_range
+                    lay_out("scalar", b, 3, i0, i1)
+                    lay_out("vector", b, 0, i0, i1)
+                    lay_out("vector", b, 1, i0, i1)
+                    g0, g1 = (0, i1 - 1) if half == 0 else (i0 - 1, NI - 1)
+                    y_out = out[b].rearrange("c (i h) z -> c (i h z)", h=HS)[:, 3 * W : 3 * W + (NI - 1) * HS * W]
+                    y_in = staged[b][:].rearrange("p i h j w -> p (i h j w)")[:, 3 * W : 3 * W + (NI - 1) * HS * W]
                     nc.sync.dma_start(
-                        out=out[b, :, i0 * HS : i1 * HS, :].rearrange("c y z -> c (y z)"),
-                        in_=out_sb[:, piece, b].rearrange("p i h j w -> p (i h j w)"),
+                        out=y_out.rearrange("c (g y) -> c g y", y=HS * W)[:, g0:g1, 0 : 3 * W],
+                        in_=y_in.rearrange("p (g y) -> p g y", y=HS * W)[:, g0:g1, 0 : 3 * W],
+                    )
+                for b in range(B):
+                    y0, y1 = (0, 2) if half == 0 else (H - 1, H)
+                    nc.sync.dma_start(
+                        out=out[b, :, y0:y1, :].rearrange("c y z -> c (y z)"),
+                        in_=staged[b][:].rearrange("p i h j w -> p (i h) (j w)")[:, y0:y1].rearrange("p y z -> p (y z)"),
                     )

@@ -21,7 +21,7 @@ TAPS = K * K
 W_COLS = TAPS * C
 QUANT_MAX = 4096
 H_VECTOR = (2, 2, 2, 2)
-C_FULL = 76
+C_FULL = 80
 C_A = 88
 C_B = 88
 I_STORE = NI // 2
@@ -174,8 +174,8 @@ def tile_patternconv_t_kernel(tc, x, weight, bias, grad_out, out):
                                 in_=by_place[:, h, i].rearrange("p (j e) t w -> p j t e w", e=2),
                             )
 
-            load_weights(0, 2)
-            load_weights(1, 2)
+            load_weights(0, 1)
+            load_weights(1, 1)
             load_grad(0, 0)
             load_grad(0, 1)
             load_grad(1, 0)
@@ -287,10 +287,13 @@ def tile_patternconv_t_kernel(tc, x, weight, bias, grad_out, out):
                 return keys
 
             staged = []
+            for i_range in pieces:
+                pass
 
-            def lay_out(engine, b, hy, i0, i1):
+            def lay_out(engine, piece, b, hy):
+                i0, i1 = pieces[piece]
                 src = planes[:, hy, :, i0:i1, b, :].rearrange("p w i j -> p i j w")
-                dst = staged[b][:, i0:i1, hy, :, :]
+                dst = staged[piece][:, b, :, hy, :, :]
                 if engine == "vector":
                     nc.vector.tensor_copy(out=dst, in_=src)
                 else:
@@ -325,42 +328,35 @@ def tile_patternconv_t_kernel(tc, x, weight, bias, grad_out, out):
                 quantise_job(jobs[n - 1])
                 late_work(n)
                 finished = multiply(jobs[n - 1])
-            for b in range(B):
-                out_sb = staging_pool.tile([P, NI, HS, NJ, WS], F32, align_bytes=64, name="staging")
+            for i_range in pieces:
+                out_sb = staging_pool.tile([P, B, I_STORE, HS, NJ, WS], F32, align_bytes=64, name="staging")
                 staged.append(out_sb)
             quantise_job(jobs[-1])
-            for key in finished:
-                close(key)
-            for key in run_passes(held_passes(WS - 1, 2)):
-                close(key)
-            direct = multiply(jobs[-1])
-            for b in range(B):
-                lay_out("scalar", b, 2, 0, NI)
-                nc.sync.dma_start(
-                    out=out[b].rearrange("c (i h) z -> c i h z", h=HS)[:, :, 2, :],
-                    in_=staged[b][:, :, 2].rearrange("p i j w -> p i (j w)"),
-                )
-            for key in direct:
-                close(key)
-            last_keys = run_passes([q for hy in (3, 0, 1) for q in held_passes(WS - 1, hy)])
-            for half, i_range in enumerate(pieces):
+            if jobs[-1][3] - jobs[-1][2] == K:
+                for key in finished:
+                    close(key)
+                for key in run_passes(held_passes(WS - 1, 2)):
+                    close(key)
+                direct = multiply(jobs[-1])
+                for key in direct:
+                    close(key)
+                last_keys = run_passes([q for hy in (3, 0, 1) for q in held_passes(WS - 1, hy)])
+            else:
+                for key in finished:
+                    close(key)
+                last_keys = multiply(jobs[-1])
+            for piece in range(len(pieces)):
+                for b in range(B):
+                    lay_out("scalar", piece, b, 2)
+            for piece, i_range in enumerate(pieces):
                 for key in last_keys:
                     close(key, i_range)
-                i0, i1 = i_range
                 for b in range(B):
-                    lay_out("scalar", b, 3, i0, i1)
-                    lay_out("vector", b, 0, i0, i1)
-                    lay_out("vector", b, 1, i0, i1)
-                    g0, g1 = (0, i1 - 1) if half == 0 else (i0 - 1, NI - 1)
-                    y_out = out[b].rearrange("c (i h) z -> c (i h z)", h=HS)[:, 3 * W : 3 * W + (NI - 1) * HS * W]
-                    y_in = staged[b][:].rearrange("p i h j w -> p (i h j w)")[:, 3 * W : 3 * W + (NI - 1) * HS * W]
+                    lay_out("scalar", piece, b, 3)
+                    lay_out("vector", piece, b, 0)
+                    lay_out("vector", piece, b, 1)
+                    i0, i1 = i_range
                     nc.sync.dma_start(
-                        out=y_out.rearrange("c (g y) -> c g y", y=HS * W)[:, g0:g1, 0 : 3 * W],
-                        in_=y_in.rearrange("p (g y) -> p g y", y=HS * W)[:, g0:g1, 0 : 3 * W],
-                    )
-                for b in range(B):
-                    y0, y1 = (0, 2) if half == 0 else (H - 1, H)
-                    nc.sync.dma_start(
-                        out=out[b, :, y0:y1, :].rearrange("c y z -> c (y z)"),
-                        in_=staged[b][:].rearrange("p i h j w -> p (i h) (j w)")[:, y0:y1].rearrange("p y z -> p (y z)"),
+                        out=out[b, :, i0 * HS : i1 * HS, :].rearrange("c y z -> c (y z)"),
+                        in_=staged[piece][:, b].rearrange("p i h j w -> p (i h j w)"),
                     )

@@ -21,7 +21,7 @@ TAPS = K * K
 W_COLS = TAPS * C
 QUANT_MAX = 4096
 H_VECTOR = (2, 2, 2, 2)
-C_FULL = 80
+C_FULL = 84
 C_A = 88
 C_B = 88
 I_STORE = NI // 2
@@ -33,7 +33,7 @@ BYTES = 2 * HS * WS * O * W_COLS + 2 * B * O * H * W + 4 * B * C * H * W
 def tile_patternconv_t_kernel(tc, x, weight, bias, grad_out, out):
     nc = tc.nc
     with tc.tile_pool(name="keep", bufs=1) as keep, tc.tile_pool(name="w_raw", bufs=4) as w_raw_pool, tc.tile_pool(
-        name="w_grouped", bufs=3
+        name="w_grouped", bufs=4
     ) as w_grouped_pool, tc.tile_pool(name="w_mx", bufs=6) as w_mx, tc.tile_pool(
         name="staging", bufs=2
     ) as staging_pool, tc.psum_pool(name="psum", bufs=8) as psum, tc.manual_schedule():
@@ -104,16 +104,26 @@ def tile_patternconv_t_kernel(tc, x, weight, bias, grad_out, out):
             regroup("scalar", job, 1, slice(cm, c1))
             regroup("scalar", job, 2, slice(c0, c1))
 
-        def quantise_job(job):
-            if job in quantised:
+        mx_tiles = {}
+
+        def quantise_job(job, last_tap=False):
+            if (job, last_tap) in quantised:
                 return
-            quantised.add(job)
+            quantised.add((job, last_tap))
             h, w, v0, v1 = job
             columns = (v1 - v0) * K * C
-            w_codes = w_mx.tile([P, columns], U32, align_bytes=64)
-            w_scales = w_mx.tile([P, columns], U8, align_bytes=64)
+            if job not in mx_tiles:
+                w_codes = w_mx.tile([P, columns], U32, align_bytes=64)
+                w_scales = w_mx.tile([P, columns], U8, align_bytes=64)
+                mx_tiles[job] = (w_codes, w_scales)
+            w_codes, w_scales = mx_tiles[job]
             flat = grouped_of[job][:].rearrange("p v u c t -> p (v u c t)")
             first = 0
+            if w == WS - 1:
+                if last_tap:
+                    first = (K - 1) * K * C
+                else:
+                    columns = (K - 1) * K * C
             while first < columns:
                 width = QUANT_MAX // PACK
                 while width > columns - first:
@@ -143,10 +153,11 @@ def tile_patternconv_t_kernel(tc, x, weight, bias, grad_out, out):
                 )
 
         def copy_scales_down(w):
-            nc.vector.tensor_copy(
-                out=g_scales_down[:, w::WS, I_STEP:N_PIX].bitcast(I32),
-                in_=g_scales[:, 2 * WS + w :: WS, 0 : N_PIX - I_STEP].bitcast(I32),
-            )
+            for low_place in (w, WS + w):
+                nc.vector.tensor_copy(
+                    out=g_scales_down[:, low_place, I_STEP:N_PIX].bitcast(I32),
+                    in_=g_scales[:, 2 * WS + low_place, 0 : N_PIX - I_STEP].bitcast(I32),
+                )
 
         with tc.tile_pool(name="g_raw", bufs=5) as g_raw_pool:
 
@@ -213,7 +224,6 @@ def tile_patternconv_t_kernel(tc, x, weight, bias, grad_out, out):
             load_weights(2, 1)
             load_weights(3, 1)
             quantise_grad(3, 0)
-            copy_scales_down(0)
 
         with tc.tile_pool(name="planes", bufs=1) as planes_pool:
             planes = planes_pool.tile([P, HS, WS, NI, B, NJ], F32)
@@ -281,7 +291,7 @@ def tile_patternconv_t_kernel(tc, x, weight, bias, grad_out, out):
             def multiply_held(job):
                 h, w, v0, v1 = job
                 keys = []
-                if v1 - v0 == K:
+                if w < WS - 1:
                     for hy in held_rows.get(h, ()):
                         keys += run_passes(held_passes(w, hy))
                 return keys
@@ -300,14 +310,19 @@ def tile_patternconv_t_kernel(tc, x, weight, bias, grad_out, out):
                     nc.scalar.copy(out=dst, in_=src)
 
             def late_work(n):
+                if n == 2:
+                    copy_scales_down(0)
                 if n == 4:
                     quantise_grad(3, 1)
+                if n == 5:
                     copy_scales_down(1)
                 if n == 8:
                     quantise_grad(3, 2)
+                if n == 9:
                     copy_scales_down(2)
                 if n == 12:
                     quantise_grad(3, 3)
+                if n == 13:
                     copy_scales_down(3)
 
             finished = []
@@ -332,26 +347,22 @@ def tile_patternconv_t_kernel(tc, x, weight, bias, grad_out, out):
                 out_sb = staging_pool.tile([P, B, I_STORE, HS, NJ, WS], F32, align_bytes=64, name="staging")
                 staged.append(out_sb)
             quantise_job(jobs[-1])
-            if jobs[-1][3] - jobs[-1][2] == K:
-                for key in finished:
+            w = WS - 1
+            direct = multiply(jobs[-1])
+            for job in jobs[-HS:]:
+                quantise_job(job, True)
+            for key in finished + direct:
+                if key[2] == 0:
                     close(key)
-                for key in run_passes(held_passes(WS - 1, 2)):
-                    close(key)
-                direct = multiply(jobs[-1])
-                for key in direct:
-                    close(key)
-                last_keys = run_passes([q for hy in (3, 0, 1) for q in held_passes(WS - 1, hy)])
-            else:
-                for key in finished:
-                    close(key)
-                last_keys = multiply(jobs[-1])
-            for piece in range(len(pieces)):
-                for b in range(B):
-                    lay_out("scalar", piece, b, 2)
+            by_halves = [key for key in finished if key[2] == 1] + run_passes(held_passes(w, 2))
+            by_halves += [key for key in direct if key[2] == 1]
+            for hy in (3, 0, 1):
+                by_halves += run_passes(held_passes(w, hy))
             for piece, i_range in enumerate(pieces):
-                for key in last_keys:
+                for key in by_halves:
                     close(key, i_range)
                 for b in range(B):
+                    lay_out("scalar", piece, b, 2)
                     lay_out("scalar", piece, b, 3)
                     lay_out("vector", piece, b, 0)
                     lay_out("vector", piece, b, 1)

@@ -154,7 +154,7 @@ def tile_patternconv_t_kernel(tc, x, weight, bias, grad_out, out):
 
         def copy_scales_down(w):
             for low_place in (w, WS + w):
-                nc.vector.tensor_copy(
+                nc.sync.dma_start(
                     out=g_scales_down[:, low_place, I_STEP:N_PIX].bitcast(I32),
                     in_=g_scales[:, 2 * WS + low_place, 0 : N_PIX - I_STEP].bitcast(I32),
                 )

import concourse.mybir as mybir

F32 = mybir.dt.float32
BF16 = mybir.dt.bfloat16
U32 = mybir.dt.uint32
U8 = mybir.dt.uint8
I32 = mybir.dt.int32
E4M3X4 = mybir.dt.float8_e4m3fn_x4
E5M2X4 = mybir.dt.float8_e5m2_x4

B, C, H, W, O, HS, WS, K = 2, 128, 64, 64, 512, 4, 4, 3
NI, NJ = H // HS, W // WS
P = 128
PACK = 4
N_PIX = B * NI * NJ
I_STEP = B * NJ
I_CHUNK = 4
N_CHUNKS = NI // I_CHUNK
CHUNK_COLS = I_CHUNK * I_STEP
TAPS = K * K
W_COLS = TAPS * C
QUANT_MAX = 4096
H_VECTOR = (2, 2, 2, 2)
C_FULL = 84
C_A = 88
C_B = 88
I_STORE = NI // 2

FLOPS = 2 * HS * WS * N_PIX * O * W_COLS
BYTES = 2 * HS * WS * O * W_COLS + 2 * B * O * H * W + 4 * B * C * H * W


def tile_patternconv_t_kernel(tc, x, weight, bias, grad_out, out):
    nc = tc.nc
    with tc.tile_pool(name="keep", bufs=1) as keep, tc.tile_pool(name="w_raw", bufs=4) as w_raw_pool, tc.tile_pool(
        name="w_grouped", bufs=4
    ) as w_grouped_pool, tc.tile_pool(name="w_mx", bufs=6) as w_mx, tc.tile_pool(
        name="staging", bufs=2
    ) as staging_pool, tc.psum_pool(name="psum", bufs=8) as psum, tc.manual_schedule():
        g_codes = keep.tile([P, HS * WS, I_STEP + N_PIX], U32, align_bytes=64)
        g_scales = keep.tile([P, HS * WS, N_PIX], U8, align_bytes=64)
        g_scales_down = keep.tile([P, 2 * WS, N_PIX], U8, align_bytes=64)
        nc.vector.memset(g_codes[:, :, 0:I_STEP].bitcast(I32), 0)
        nc.vector.memset(g_scales[:, 2 * WS :].bitcast(I32), 0)
        nc.vector.memset(g_scales_down[:, :, 0:I_STEP].bitcast(I32), 0)

        places = [(h, w) for w in range(WS) for h in range(HS)]
        jobs = []
        for w in range(WS):
            if w not in ():
                jobs += [(h, w, 0, K) for h in range(HS)]
            else:
                jobs += [(h, w, 0, K - 1) for h in range(HS)] + [(h, w, K - 1, K) for h in range(HS)]
        w_raw_of = {}
        grouped_of = {}
        w_mx_of = {}
        quantised = set()

        def load_weights(n, parts=1):
            h, w = places[n]
            w_raw = w_raw_pool.tile([P, PACK, C, K, K], BF16)
            for part in range(parts):
                channels = slice(part * C // parts, (part + 1) * C // parts)
                nc.sync.dma_start(
                    out=w_raw[:, :, channels].rearrange("p t c u v -> p t (c u v)"),
                    in_=weight[h, w, :, channels].rearrange("(p t) c u v -> p t (c u v)", t=PACK),
                )
            w_raw_of[(h, w)] = w_raw

        def load_up_to(n):
            while len(w_raw_of) <= min(n, len(places) - 1):
                load_weights(len(w_raw_of))

        def regroup(engine, job, u, channels):
            h, w, v0, v1 = job
            run = 2 if v1 - v0 == K else 4
            out_view = grouped_of[job][:, :, u, channels, :].rearrange("p v (c e) t -> p c t e v", e=run)
            in_view = w_raw_of[(h, w)][:, :, channels, u, v0:v1].rearrange("p t (c e) v -> p c t e v", e=run)
            if engine == "vector":
                nc.vector.tensor_copy(out=out_view, in_=in_view)
            else:
                nc.scalar.copy(out=out_view, in_=in_view)

        def grouped_tile(job):
            if job not in grouped_of:
                w_grouped = w_grouped_pool.tile([P, job[3] - job[2], K, C, PACK], BF16, align_bytes=64)
                grouped_of[job] = w_grouped

        def share(job):
            return {K: C_FULL, K - 1: C_A, 1: C_B}[job[3] - job[2]]

        def regroup_vector(job):
            grouped_tile(job)
            regroup("vector", job, 0, slice(0, C))
            if share(job) > 0:
                regroup("vector", job, 1, slice(0, share(job)))

        def regroup_whole(n, c0, c1):
            job = jobs[n]
            grouped_tile(job)
            cm = c0 + (c1 - c0) * C_FULL // C // 2 * 2
            regroup("vector", job, 0, slice(c0, c1))
            regroup("vector", job, 1, slice(c0, cm))
            regroup("scalar", job, 1, slice(cm, c1))
            regroup("scalar", job, 2, slice(c0, c1))

        mx_tiles = {}

        def quantise_job(job, last_tap=False):
            if (job, last_tap) in quantised:
                return
            quantised.add((job, last_tap))
            h, w, v0, v1 = job
            columns = (v1 - v0) * K * C
            if job not in mx_tiles:
                w_codes = w_mx.tile([P, columns], U32, align_bytes=64)
                w_scales = w_mx.tile([P, columns], U8, align_bytes=64)
                mx_tiles[job] = (w_codes, w_scales)
            w_codes, w_scales = mx_tiles[job]
            flat = grouped_of[job][:].rearrange("p v u c t -> p (v u c t)")
            first = 0
            if w == WS - 1:
                if last_tap:
                    first = (K - 1) * K * C
                else:
                    columns = (K - 1) * K * C
            while first < columns:
                width = QUANT_MAX // PACK
                while width > columns - first:
                    width = width // 2
                nc.vector.quantize_mx(
                    out=w_codes[:, first : first + width].bitcast(E4M3X4),
                    scales=w_scales[:, first : first + width],
                    in_=flat[:, first * PACK : (first + width) * PACK],
                )
                first += width
            for v in range(v0, v1):
                for u in range(K):
                    tap = slice(((v - v0) * K + u) * C, ((v - v0) * K + u + 1) * C)
                    w_mx_of[(h, w, u, v)] = (w_codes[:, tap], w_scales[:, tap])

        g_raw_of = {}
        g_grouped_of = {}

        def quantise_grad(m, w):
            cols = slice(m * CHUNK_COLS, (m + 1) * CHUNK_COLS)
            padded_cols = slice(I_STEP + m * CHUNK_COLS, I_STEP + (m + 1) * CHUNK_COLS)
            for h in range(HS):
                nc.vector.quantize_mx(
                    out=g_codes[:, h * WS + w, padded_cols].bitcast(E5M2X4),
                    scales=g_scales[:, h * WS + w, cols],
                    in_=g_grouped_of[m][:, h, w].rearrange("p i b j t -> p (i b j t)"),
                )

        def copy_scales_down(w):
            for low_place in (w, WS + w):
                nc.sync.dma_start(
                    out=g_scales_down[:, low_place, I_STEP:N_PIX].bitcast(I32),
                    in_=g_scales[:, 2 * WS + low_place, 0 : N_PIX - I_STEP].bitcast(I32),
                )

        with tc.tile_pool(name="g_raw", bufs=5) as g_raw_pool:

            def load_grad(m, b):
                rows = slice(m * I_CHUNK * HS, (m + 1) * I_CHUNK * HS)
                g_raw = g_raw_pool.tile([P, PACK, I_CHUNK * HS * W], BF16)
                nc.sync.dma_start(
                    out=g_raw[:], in_=grad_out[b, :, rows, :].rearrange("(p t) y z -> p t (y z)", t=PACK)
                )
                g_raw_of[(m, b)] = g_raw

            def regroup_grad(m, b):
                if b == 0:
                    g_grouped = staging_pool.tile([P, HS, WS, I_CHUNK, B, NJ, PACK], BF16, align_bytes=64, name="staging")
                    g_grouped_of[m] = g_grouped
                by_place = g_raw_of[(m, b)][:].rearrange("p t (i h j w) -> p h i j t w", i=I_CHUNK, h=HS, j=NJ, w=WS)
                for h in range(HS):
                    dst = g_grouped_of[m][:, h, :, :, b, :, :].rearrange("p w i j t -> p i j t w")
                    if h < H_VECTOR[m]:
                        nc.vector.tensor_copy(out=dst, in_=by_place[:, h])
                    else:
                        for i in range(I_CHUNK):
                            nc.scalar.copy(
                                out=dst[:, i].rearrange("p (j e) t w -> p j t e w", e=2),
                                in_=by_place[:, h, i].rearrange("p (j e) t w -> p j t e w", e=2),
                            )

            load_weights(0, 1)
            load_weights(1, 1)
            load_grad(0, 0)
            load_grad(0, 1)
            load_grad(1, 0)
            regroup_whole(0, 0, C // 2)
            regroup_whole(0, C // 2, C)
            regroup_whole(1, 0, C // 2)
            quantise_job(jobs[0])
            regroup_whole(1, C // 2, C)
            regroup_grad(0, 0)
            quantise_job(jobs[1])
            regroup_grad(0, 1)
            load_grad(1, 1)
            regroup_grad(1, 0)
            quantise_grad(0, 0)
            quantise_grad(0, 1)
            regroup_grad(1, 1)
            quantise_grad(0, 2)
            quantise_grad(0, 3)
            load_grad(2, 0)
            regroup_grad(2, 0)
            quantise_grad(1, 0)
            quantise_grad(1, 1)
            load_grad(2, 1)
            regroup_grad(2, 1)
            quantise_grad(1, 2)
            quantise_grad(1, 3)
            load_grad(3, 0)
            regroup_grad(3, 0)
            quantise_grad(2, 0)
            quantise_grad(2, 1)
            load_grad(3, 1)
            regroup_grad(3, 1)
            quantise_grad(2, 2)
            quantise_grad(2, 3)
            load_weights(2, 1)
            load_weights(3, 1)
            quantise_grad(3, 0)

        with tc.tile_pool(name="planes", bufs=1) as planes_pool:
            planes = planes_pool.tile([P, HS, WS, NI, B, NJ], F32)
            whole = (0, NI)
            pieces = [(i_first, i_first + I_STORE) for i_first in range(0, NI, I_STORE)]
            acc_of = {}
            passes_done = {}

            def close(key, i_range=whole):
                hy, wz, dj = key
                i0, i1 = i_range
                plane = planes[:, hy, wz, i0:i1]
                acc = acc_of[key][:, i0 * I_STEP : i1 * I_STEP]
                if dj == 0:
                    nc.scalar.copy(out=plane.rearrange("p i b j -> p (i b j)"), in_=acc)
                else:
                    shifted = acc.rearrange("p (i b j) -> p i b j", i=i1 - i0, b=B)
                    nc.vector.tensor_add(
                        out=plane[:, :, :, 1:NJ], in0=shifted[:, :, :, 0 : NJ - 1], in1=plane[:, :, :, 1:NJ]
                    )

            def run_pass(h, w, u, v):
                w_codes, w_scales = w_mx_of[(h, w, u, v)]
                hy, di = (h + u) % HS, (h + u) // HS
                wz, dj = (w + v) % WS, (w + v) // WS
                key = (hy, wz, dj)
                source_columns = min(wz + 1, K) if dj == 0 else K - 1 - wz
                if key not in acc_of:
                    acc = psum.tile([P, N_PIX], F32)
                    acc_of[key] = acc
                    passes_done[key] = 0
                place = h * WS + w
                if di == 0:
                    rhs = g_codes[:, place, I_STEP : I_STEP + N_PIX]
                    rhs_scale = g_scales[:, place, :]
                else:
                    rhs = g_codes[:, place, 0:N_PIX]
                    rhs_scale = g_scales_down[:, place - 2 * WS, :]
                passes_done[key] += 1
                full = passes_done[key] == K * source_columns
                nc.tensor.matmul_mx(
                    out=acc_of[key][:],
                    lhsT=w_codes.bitcast(E4M3X4),
                    lhsT_scale=w_scales,
                    rhs=rhs.bitcast(E5M2X4),
                    rhs_scale=rhs_scale,
                    start=(passes_done[key] == 1),
                    stop=full,
                )
                return [key] if full else []

            def run_passes(passes):
                return [key for one in passes for key in run_pass(*one)]

            def held_passes(w, hy):
                return [(h, w, (hy - h) % HS, K - 1) for h in range(HS) if (hy - h) % HS < K]

            held_rows = {2: (2,), 3: (3, 0, 1)}

            def multiply(job):
                h, w, v0, v1 = job
                taps = range(v0, v1) if v1 - v0 < K else range(v0, K - 1)
                return run_passes([(h, w, u, v) for v in taps for u in range(K)])

            def multiply_held(job):
                h, w, v0, v1 = job
                keys = []
                if w < WS - 1:
                    for hy in held_rows.get(h, ()):
                        keys += run_passes(held_passes(w, hy))
                return keys

            staged = []
            for i_range in pieces:
                pass

            def lay_out(engine, piece, b, hy):
                i0, i1 = pieces[piece]
                src = planes[:, hy, :, i0:i1, b, :].rearrange("p w i j -> p i j w")
                dst = staged[piece][:, b, :, hy, :, :]
                if engine == "vector":
                    nc.vector.tensor_copy(out=dst, in_=src)
                else:
                    nc.scalar.copy(out=dst, in_=src)

            def late_work(n):
                if n == 2:
                    copy_scales_down(0)
                if n == 4:
                    quantise_grad(3, 1)
                if n == 5:
                    copy_scales_down(1)
                if n == 8:
                    quantise_grad(3, 2)
                if n == 9:
                    copy_scales_down(2)
                if n == 12:
                    quantise_grad(3, 3)
                if n == 13:
                    copy_scales_down(3)

            finished = []
            first = 2
            for n in range(first - 1):
                finished += multiply(jobs[n])
            for n in range(first, len(jobs)):
                job = jobs[n]
                load_up_to(places.index(job[:2]) + 2)
                regroup_vector(job)
                regroup("scalar", job, 2, slice(0, C))
                for key in finished:
                    close(key)
                if n > 1:
                    multiply_held(jobs[n - 2])
                if share(job) < C:
                    regroup("scalar", job, 1, slice(share(job), C))
                quantise_job(jobs[n - 1])
                late_work(n)
                finished = multiply(jobs[n - 1])
            for i_range in pieces:
                out_sb = staging_pool.tile([P, B, I_STORE, HS, NJ, WS], F32, align_bytes=64, name="staging")
                staged.append(out_sb)
            quantise_job(jobs[-1])
            w = WS - 1
            direct = multiply(jobs[-1])
            for job in jobs[-HS:]:
                quantise_job(job, True)
            for key in finished + direct:
                if key[2] == 0:
                    close(key)
            by_halves = [key for key in finished if key[2] == 1] + run_passes(held_passes(w, 2))
            by_halves += [key for key in direct if key[2] == 1]
            for hy in (3, 0, 1):
                by_halves += run_passes(held_passes(w, hy))
            for piece, i_range in enumerate(pieces):
                for key in by_halves:
                    close(key, i_range)
                for b in range(B):
                    lay_out("scalar", piece, b, 2)
                    lay_out("scalar", piece, b, 3)
                    lay_out("vector", piece, b, 0)
                    lay_out("vector", piece, b, 1)
                    i0, i1 = i_range
                    nc.sync.dma_start(
                        out=out[b, :, i0 * HS : i1 * HS, :].rearrange("c y z -> c (y z)"),
                        in_=staged[piece][:, b].rearrange("p i h j w -> p (i h j w)"),
                    )
